import numpy as np
import ml_dtypes


def mxq(x, axis, fmt="e4m3"):
    dtype, down = {"e4m3": (ml_dtypes.float8_e4m3fn, 7), "e5m2": (ml_dtypes.float8_e5m2, 14)}[fmt]
    v = np.moveaxis(np.asarray(x, np.float32).astype(ml_dtypes.bfloat16).astype(np.float64), axis, -1)
    blocks = v.reshape(v.shape[:-1] + (-1, 32))
    amax = np.abs(blocks).max(-1, keepdims=True)
    byte = np.maximum(np.where(amax > 0, np.frexp(amax)[1] - 1 + 127, 0) - down, 1)
    scale = np.exp2(byte - 127.0)
    codes = (blocks / scale).astype(np.float32).astype(dtype).astype(np.float64)
    return np.moveaxis((codes * scale).reshape(v.shape), -1, axis)


WIDE = False


def mx_kscale(k):
    if not WIDE:
        return np.ones(k)
    levels = np.array([10, -10, 5, -5, 0])
    a = np.random.permutation(np.resize(levels, k // 512 * 4)).reshape(k // 512, 4)
    idx = np.arange(k)
    return np.exp2(a[idx // 512, idx % 128 // 32])


BF16 = ml_dtypes.bfloat16


def bf(x):
    return np.asarray(x, np.float32).astype(BF16)


def f64(x):
    return np.asarray(x).astype(np.float64)


L, B, D, D0 = 512, 4, 1024, 768
EPS_BN = 1e-5
EPS_LN = 1e-5


def setup_inputs():
    n = np.random.standard_normal
    s = mx_kscale(D)
    r = n((B, L, D))
    return {"x": bf(n((L, B, D))), "res_a": bf(np.where(r > 0, r, 0.25 * r)),
            "ctx_v": bf(n((B, L, D)) * 0.25 * s), "W_v": bf(n((D, D)) * 2.0 / np.sqrt(D) / s[None, :]),
            "bn_v_g": bf(1.0 + 0.1 * n(D)), "bn_v_b": bf(0.2 * n(D)),
            "prelu_v": bf(0.25 + 0.05 * n(1)), "ln_g": bf(1.0 + 0.1 * n(D)), "ln_b": bf(0.2 * n(D))}


def reference(x, res_a, ctx_v, W_v, bn_v_g, bn_v_b, prelu_v, ln_g, ln_b):
    xq = np.swapaxes(f64(x), 0, 1)
    y = mxq(f64(ctx_v), 2, "e4m3") @ mxq(f64(W_v), 1, "e4m3").T
    mean = y.mean(axis=(0, 1))
    var = y.var(axis=(0, 1))
    z = (y - mean) / np.sqrt(var + EPS_BN) * f64(bn_v_g) + f64(bn_v_b)
    res_v = np.where(z > 0, z, f64(prelu_v) * z)
    out = np.swapaxes(xq + f64(res_a) + res_v, 0, 1)
    mu = out.mean(axis=-1, keepdims=True)
    v = out.var(axis=-1, keepdims=True)
    return (out - mu) / np.sqrt(v + EPS_LN) * f64(ln_g) + f64(ln_b)

@@ -1,0 +1,198 @@
+from contextlib import ExitStack
+
+import concourse.mybir as mybir
+from concourse.masks import make_identity
+
+F32 = mybir.dt.float32
+BF16 = mybir.dt.bfloat16
+U32 = mybir.dt.uint32
+U8 = mybir.dt.uint8
+FP8X4 = mybir.dt.float8_e4m3fn_x4
+ALU = mybir.AluOpType
+ACT = mybir.ActivationFunctionType
+
+P = 128
+L, B, D = 512, 4, 1024
+PASSES = 2
+GROUP = 512
+TILES = GROUP // P
+L_TILES = L // P
+W_GROUPS = D // GROUP
+C_TILES = D // P
+BANK = 512
+HALVES = D // BANK
+EPS = 1e-5
+
+FLOPS = 2 * L * B * D * D
+
+
+def quantise_group(nc, stage, psum_t, ident, rows, codes, scales):
+    raw = stage.tile([P, TILES, D], BF16)
+    nc.sync.dma_start(out=raw[:], in_=rows)
+    grouped = stage.tile([P, PASSES * GROUP * 4], BF16, align_bytes=64)
+    grouped_words = grouped[:].bitcast(F32).rearrange("p (g r u) -> p g r u", g=PASSES, u=2)
+    for r in range(TILES):
+        words = raw[:, r, :].bitcast(F32)
+        xt = psum_t.tile([P, PASSES, 2, P], F32, tag="xt")
+        for g in range(PASSES):
+            for u in range(2):
+                first = (2 * g + u) * P
+                nc.tensor.transpose(xt[:, g, u, :], words[:, first : first + P], ident[:])
+        nc.scalar.copy(
+            out=grouped_words[:, :, r * P : (r + 1) * P, :],
+            in_=xt[:].rearrange("p g u r -> p g r u"),
+        )
+    nc.vector.quantize_mx(
+        out=codes.rearrange("p g r -> p (g r)").bitcast(FP8X4),
+        scales=scales.rearrange("p g r -> p (g r)"),
+        in_=grouped[:],
+    )
+
+
+def product_tile(nc, psum_y, w_codes, w_scales, c_codes, c_scales, ct):
+    h, q = divmod(ct, TILES)
+    cols = slice(q * P, (q + 1) * P)
+    y = psum_y.tile([P, GROUP], F32, tag="y")
+    for g in range(PASSES):
+        nc.tensor.matmul_mx(
+            out=y[:],
+            lhsT=w_codes[h][:, g, cols].bitcast(FP8X4),
+            lhsT_scale=w_scales[h][:, g, cols],
+            rhs=c_codes[:, g, :].bitcast(FP8X4),
+            rhs_scale=c_scales[:, g, :],
+            start=(g == 0),
+            stop=(g == PASSES - 1),
+        )
+    return y
+
+
+def tile_coattention_pb_kernel(tc, x, res_a, ctx_v, W_v, bn_v_g, bn_v_b, prelu_v, ln_g, ln_b, out):
+    nc = tc.nc
+    with ExitStack() as whole:
+        const = whole.enter_context(tc.tile_pool(name="const", bufs=1))
+        keep = whole.enter_context(tc.tile_pool(name="keep", bufs=1))
+        streams = whole.enter_context(tc.tile_pool(name="streams", bufs=2))
+        psum_y = whole.enter_context(tc.psum_pool(name="psum_y", bufs=4))
+
+        ident = const.tile([P, P], F32)
+        make_identity(nc, ident[:])
+        ident_bf = const.tile([P, P], BF16)
+        make_identity(nc, ident_bf[:])
+        eps = const.tile([P, 1], F32)
+        nc.vector.memset(eps[:], EPS)
+
+        bn_rows = const.tile([P, P], BF16)
+        nc.vector.memset(bn_rows[:], 0.0)
+        nc.sync.dma_start(out=bn_rows[0:C_TILES, :], in_=bn_v_g.rearrange("(t c) -> t c", t=C_TILES))
+        nc.sync.dma_start(out=bn_rows[C_TILES : 2 * C_TILES, :], in_=bn_v_b.rearrange("(t c) -> t c", t=C_TILES))
+        slope = const.tile([P, 1], BF16)
+        nc.sync.dma_start(out=slope[:], in_=prelu_v.partition_broadcast(P))
+        slope_less_1 = const.tile([P, 1], F32)
+        nc.vector.tensor_scalar_add(out=slope_less_1[:], in0=slope[:], scalar1=-1.0)
+
+        w_codes = [keep.tile([P, PASSES, GROUP], U32, align_bytes=64, name="w_codes%d" % h) for h in range(W_GROUPS)]
+        w_scales = [keep.tile([P, PASSES, GROUP], U8, align_bytes=64, name="w_scales%d" % h) for h in range(W_GROUPS)]
+        c_codes = [keep.tile([P, PASSES, GROUP], U32, align_bytes=64, name="c_codes%d" % j) for j in range(L_TILES)]
+        c_scales = [keep.tile([P, PASSES, GROUP], U8, align_bytes=64, name="c_scales%d" % j) for j in range(L_TILES)]
+        stats = keep.tile([P, C_TILES, L_TILES, 6], F32)
+
+        with tc.tile_pool(name="stage", bufs=2) as stage, tc.psum_pool(name="psum_t", bufs=4) as psum_t:
+            bn_cols = psum_t.tile([P, P], BF16, tag="xt")
+            nc.tensor.transpose(bn_cols[:], bn_rows[:], ident_bf[:])
+            bn_gain_bias = const.tile([P, 2 * C_TILES], F32)
+            nc.vector.tensor_copy(out=bn_gain_bias[:], in_=bn_cols[:, 0 : 2 * C_TILES])
+
+            for h in range(W_GROUPS):
+                rows = W_v[h * GROUP : (h + 1) * GROUP, :].rearrange("(r p) k -> p r k", p=P)
+                quantise_group(nc, stage, psum_t, ident, rows, w_codes[h][:], w_scales[h][:])
+            for j in range(L_TILES):
+                rows = ctx_v[:, j * P : (j + 1) * P, :].rearrange("b l k -> l b k")
+                quantise_group(nc, stage, psum_t, ident, rows, c_codes[j][:], c_scales[j][:])
+                for ct in range(C_TILES):
+                    y = product_tile(nc, psum_y, w_codes, w_scales, c_codes[j], c_scales[j], ct)
+                    nc.vector.bn_stats(out=stats[:, ct, j, :], in_=y[:])
+
+        xa = []
+        for j in range(L_TILES):
+            x_t = streams.tile([P, B, D], BF16)
+            nc.sync.dma_start(out=x_t[:], in_=x[j * P : (j + 1) * P, :, :])
+            a_t = streams.tile([P, B, D], BF16)
+            nc.sync.dma_start(out=a_t[:], in_=res_a[:, j * P : (j + 1) * P, :].rearrange("b l c -> l b c"))
+            xa_j = keep.tile([P, B, D], F32, name="xa%d" % j)
+            for b in range(B):
+                nc.gpsimd.tensor_tensor(out=xa_j[:, b, :], in0=x_t[:, b, :], in1=a_t[:, b, :], op=ALU.add)
+            xa.append(xa_j)
+        ln_gain = const.tile([P, D], BF16)
+        nc.sync.dma_start(out=ln_gain[:], in_=ln_g.partition_broadcast(P))
+        ln_bias = const.tile([P, D], BF16)
+        nc.sync.dma_start(out=ln_bias[:], in_=ln_b.partition_broadcast(P))
+
+        mean_var = keep.tile([P, C_TILES, 2], F32)
+        for ct in range(C_TILES):
+            nc.vector.bn_aggr(out=mean_var[:, ct, :], in_=stats[:, ct, :, :].rearrange("p j s -> p (j s)"))
+        bn_rstd = keep.tile([P, C_TILES], F32)
+        nc.scalar.activation(out=bn_rstd[:], in_=mean_var[:, :, 1], func=ACT.Abs_reciprocal_sqrt, bias=eps[:], scale=1.0)
+        bn_scale = keep.tile([P, C_TILES], F32)
+        nc.vector.tensor_mul(out=bn_scale[:], in0=bn_rstd[:], in1=bn_gain_bias[:, 0:C_TILES])
+        bn_shift = keep.tile([P, C_TILES], F32)
+        nc.vector.tensor_mul(out=bn_shift[:], in0=mean_var[:, :, 0], in1=bn_scale[:])
+        nc.vector.tensor_sub(out=bn_shift[:], in0=bn_gain_bias[:, C_TILES : 2 * C_TILES], in1=bn_shift[:])
+
+        row_sum = keep.tile([P, L_TILES * B, HALVES], F32)
+        neg_mean = keep.tile([P, L_TILES * B], F32)
+        sum_sq = keep.tile([P, L_TILES * B], F32)
+        ln_rstd = keep.tile([P, L_TILES * B], F32)
+        with ExitStack() as second:
+            chan = second.enter_context(tc.tile_pool(name="chan", bufs=2 * C_TILES))
+            rowp = second.enter_context(tc.tile_pool(name="rowp", bufs=4))
+            psum_o = second.enter_context(tc.psum_pool(name="psum_o", bufs=4))
+            for j in range(L_TILES):
+                z_tiles = []
+                n_tiles = []
+                for ct in range(C_TILES):
+                    y = product_tile(nc, psum_y, w_codes, w_scales, c_codes[j], c_scales[j], ct)
+                    z = chan.tile([P, GROUP], F32)
+                    nc.scalar.activation(
+                        out=z[:], in_=y[:], func=ACT.Identity, bias=bn_shift[:, ct : ct + 1], scale=bn_scale[:, ct : ct + 1]
+                    )
+                    n = chan.tile([P, GROUP], F32)
+                    nc.vector.tensor_scalar(
+                        out=n[:], in0=z[:], scalar1=0.0, scalar2=slope_less_1[:], op0=ALU.min, op1=ALU.mult
+                    )
+                    z_tiles.append(z)
+                    n_tiles.append(n)
+                for b in range(B):
+                    i = j * B + b
+                    rows = slice(b * P, (b + 1) * P)
+                    o = xa[j][:, b, :]
+                    for half in range(HALVES):
+                        res_v = psum_o.tile([P, BANK], F32)
+                        for q in range(TILES):
+                            ct = half * TILES + q
+                            cells = res_v[:, q * P : (q + 1) * P]
+                            nc.tensor.matmul(cells, lhsT=z_tiles[ct][:, rows], rhs=ident[:], is_transpose=True, start=True, stop=False)
+                            nc.tensor.matmul(cells, lhsT=n_tiles[ct][:, rows], rhs=ident[:], is_transpose=True, start=False, stop=True)
+                        cols = slice(half * BANK, (half + 1) * BANK)
+                        nc.vector.scalar_tensor_tensor(
+                            out=o[:, cols], in0=res_v[:], scalar=1.0, in1=o[:, cols], op0=ALU.mult, op1=ALU.add,
+                            accum_out=row_sum[:, i, half : half + 1],
+                        )
+                    nc.vector.tensor_scalar(
+                        out=neg_mean[:, i : i + 1], in0=row_sum[:, i, 0:1], scalar1=row_sum[:, i, 1:2], scalar2=-1.0 / D,
+                        op0=ALU.add, op1=ALU.mult,
+                    )
+                    squares = rowp.tile([P, D], BF16)
+                    nc.scalar.activation(
+                        out=squares[:], in_=o, func=ACT.Square, bias=neg_mean[:, i : i + 1], scale=1.0,
+                        accum_out=sum_sq[:, i : i + 1],
+                    )
+                    nc.scalar.activation(
+                        out=ln_rstd[:, i : i + 1], in_=sum_sq[:, i : i + 1], func=ACT.Abs_reciprocal_sqrt, bias=eps[:], scale=1.0 / D
+                    )
+                    res = rowp.tile([P, D], F32)
+                    nc.vector.scalar_tensor_tensor(
+                        out=res[:], in0=o, scalar=neg_mean[:, i : i + 1], in1=ln_gain[:], op0=ALU.add, op1=ALU.mult
+                    )
+                    nc.scalar.activation(out=res[:], in_=res[:], func=ACT.Copy, scale=ln_rstd[:, i : i + 1])
+                    nc.gpsimd.tensor_tensor(out=res[:], in0=res[:], in1=ln_bias[:], op=ALU.add)
+                    nc.sync.dma_start(out=out[j * P : (j + 1) * P, b, :], in_=res[:])

@@ -26,8 +26,8 @@ EPS = 1e-5
 FLOPS = 2 * L * B * D * D
 
 
-def quantise_group(nc, stage, psum_t, ident, rows, codes, scales):
-    raw = stage.tile([P, TILES, D], BF16)
+def quantise_group(nc, raws, stage, psum_t, ident, rows, codes, scales):
+    raw = raws.tile([P, TILES, D], BF16)
     nc.sync.dma_start(out=raw[:], in_=rows)
     grouped = stage.tile([P, PASSES * GROUP * 4], BF16, align_bytes=64)
     grouped_words = grouped[:].bitcast(F32).rearrange("p (g r u) -> p g r u", g=PASSES, u=2)
@@ -69,6 +69,7 @@ def product_tile(nc, psum_y, w_codes, w_scales, c_codes, c_scales, ct):
 def tile_coattention_pb_kernel(tc, x, res_a, ctx_v, W_v, bn_v_g, bn_v_b, prelu_v, ln_g, ln_b, out):
     nc = tc.nc
     with ExitStack() as whole:
+        whole.enter_context(tc.manual_schedule())
         const = whole.enter_context(tc.tile_pool(name="const", bufs=1))
         keep = whole.enter_context(tc.tile_pool(name="keep", bufs=1))
         streams = whole.enter_context(tc.tile_pool(name="streams", bufs=2))
@@ -80,6 +81,8 @@ def tile_coattention_pb_kernel(tc, x, res_a, ctx_v, W_v, bn_v_g, bn_v_b, prelu_v
         make_identity(nc, ident_bf[:])
         eps = const.tile([P, 1], F32)
         nc.vector.memset(eps[:], EPS)
+        table_first = const.tile([P, 1], F32)
+        nc.scalar.activation(out=table_first[:], in_=eps[:], func=ACT.Abs_reciprocal_sqrt)
 
         bn_rows = const.tile([P, P], BF16)
         nc.vector.memset(bn_rows[:], 0.0)
@@ -96,7 +99,15 @@ def tile_coattention_pb_kernel(tc, x, res_a, ctx_v, W_v, bn_v_g, bn_v_b, prelu_v
         c_scales = [keep.tile([P, PASSES, GROUP], U8, align_bytes=64, name="c_scales%d" % j) for j in range(L_TILES)]
         stats = keep.tile([P, C_TILES, L_TILES, 6], F32)
 
-        with tc.tile_pool(name="stage", bufs=2) as stage, tc.psum_pool(name="psum_t", bufs=4) as psum_t:
+        with ExitStack() as first:
+            raws = first.enter_context(tc.tile_pool(name="raws", bufs=3))
+            stage = first.enter_context(tc.tile_pool(name="stage", bufs=2))
+            psum_t = first.enter_context(tc.psum_pool(name="psum_t", bufs=4))
+
+            def quantise_ctx(j):
+                rows = ctx_v[:, j * P : (j + 1) * P, :].rearrange("b l k -> l b k")
+                quantise_group(nc, raws, stage, psum_t, ident, rows, c_codes[j][:], c_scales[j][:])
+
             bn_cols = psum_t.tile([P, P], BF16, tag="xt")
             nc.tensor.transpose(bn_cols[:], bn_rows[:], ident_bf[:])
             bn_gain_bias = const.tile([P, 2 * C_TILES], F32)
@@ -104,10 +115,11 @@ def tile_coattention_pb_kernel(tc, x, res_a, ctx_v, W_v, bn_v_g, bn_v_b, prelu_v
 
             for h in range(W_GROUPS):
                 rows = W_v[h * GROUP : (h + 1) * GROUP, :].rearrange("(r p) k -> p r k", p=P)
-                quantise_group(nc, stage, psum_t, ident, rows, w_codes[h][:], w_scales[h][:])
+                quantise_group(nc, raws, stage, psum_t, ident, rows, w_codes[h][:], w_scales[h][:])
+            quantise_ctx(0)
             for j in range(L_TILES):
-                rows = ctx_v[:, j * P : (j + 1) * P, :].rearrange("b l k -> l b k")
-                quantise_group(nc, stage, psum_t, ident, rows, c_codes[j][:], c_scales[j][:])
+                if j + 1 < L_TILES:
+                    quantise_ctx(j + 1)
                 for ct in range(C_TILES):
                     y = product_tile(nc, psum_y, w_codes, w_scales, c_codes[j], c_scales[j], ct)
                     nc.vector.bn_stats(out=stats[:, ct, j, :], in_=y[:])
@@ -144,55 +156,77 @@ def tile_coattention_pb_kernel(tc, x, res_a, ctx_v, W_v, bn_v_g, bn_v_b, prelu_v
         ln_rstd = keep.tile([P, L_TILES * B], F32)
         with ExitStack() as second:
             chan = second.enter_context(tc.tile_pool(name="chan", bufs=2 * C_TILES))
-            rowp = second.enter_context(tc.tile_pool(name="rowp", bufs=4))
+            junk = second.enter_context(tc.tile_pool(name="junk", bufs=2))
+            rowp = second.enter_context(tc.tile_pool(name="rowp", bufs=5))
             psum_o = second.enter_context(tc.psum_pool(name="psum_o", bufs=4))
-            for j in range(L_TILES):
-                z_tiles = []
-                n_tiles = []
-                for ct in range(C_TILES):
-                    y = product_tile(nc, psum_y, w_codes, w_scales, c_codes[j], c_scales[j], ct)
-                    z = chan.tile([P, GROUP], F32)
-                    nc.scalar.activation(
-                        out=z[:], in_=y[:], func=ACT.Identity, bias=bn_shift[:, ct : ct + 1], scale=bn_scale[:, ct : ct + 1]
-                    )
-                    n = chan.tile([P, GROUP], F32)
-                    nc.vector.tensor_scalar(
-                        out=n[:], in0=z[:], scalar1=0.0, scalar2=slope_less_1[:], op0=ALU.min, op1=ALU.mult
-                    )
-                    z_tiles.append(z)
-                    n_tiles.append(n)
-                for b in range(B):
-                    i = j * B + b
-                    rows = slice(b * P, (b + 1) * P)
-                    o = xa[j][:, b, :]
-                    for half in range(HALVES):
-                        res_v = psum_o.tile([P, BANK], F32)
-                        for q in range(TILES):
-                            ct = half * TILES + q
-                            cells = res_v[:, q * P : (q + 1) * P]
-                            nc.tensor.matmul(cells, lhsT=z_tiles[ct][:, rows], rhs=ident[:], is_transpose=True, start=True, stop=False)
-                            nc.tensor.matmul(cells, lhsT=n_tiles[ct][:, rows], rhs=ident[:], is_transpose=True, start=False, stop=True)
-                        cols = slice(half * BANK, (half + 1) * BANK)
-                        nc.vector.scalar_tensor_tensor(
-                            out=o[:, cols], in0=res_v[:], scalar=1.0, in1=o[:, cols], op0=ALU.mult, op1=ALU.add,
-                            accum_out=row_sum[:, i, half : half + 1],
-                        )
-                    nc.vector.tensor_scalar(
-                        out=neg_mean[:, i : i + 1], in0=row_sum[:, i, 0:1], scalar1=row_sum[:, i, 1:2], scalar2=-1.0 / D,
-                        op0=ALU.add, op1=ALU.mult,
-                    )
-                    squares = rowp.tile([P, D], BF16)
-                    nc.scalar.activation(
-                        out=squares[:], in_=o, func=ACT.Square, bias=neg_mean[:, i : i + 1], scale=1.0,
-                        accum_out=sum_sq[:, i : i + 1],
-                    )
-                    nc.scalar.activation(
-                        out=ln_rstd[:, i : i + 1], in_=sum_sq[:, i : i + 1], func=ACT.Abs_reciprocal_sqrt, bias=eps[:], scale=1.0 / D
-                    )
-                    res = rowp.tile([P, D], F32)
+            z_tiles = {}
+            n_tiles = {}
+            res_tiles = {}
+
+            def batch_norm_prelu(j, ct):
+                y = product_tile(nc, psum_y, w_codes, w_scales, c_codes[j], c_scales[j], ct)
+                z = chan.tile([P, GROUP], F32)
+                nc.scalar.activation(
+                    out=z[:], in_=y[:], func=ACT.Identity, bias=bn_shift[:, ct : ct + 1], scale=bn_scale[:, ct : ct + 1]
+                )
+                n = chan.tile([P, GROUP], F32)
+                nc.vector.tensor_scalar(out=n[:], in0=z[:], scalar1=0.0, scalar2=slope_less_1[:], op0=ALU.min, op1=ALU.mult)
+                z_tiles[j, ct] = z
+                n_tiles[j, ct] = n
+
+            def sum_of_streams(j, b):
+                i = j * B + b
+                rows = slice(b * P, (b + 1) * P)
+                for half in range(HALVES):
+                    res_v = psum_o.tile([P, BANK], F32)
+                    for q in range(TILES):
+                        ct = half * TILES + q
+                        cells = res_v[:, q * P : (q + 1) * P]
+                        nc.tensor.matmul(cells, lhsT=z_tiles[j, ct][:, rows], rhs=ident[:], is_transpose=True, start=True, stop=False)
+                        nc.tensor.matmul(cells, lhsT=n_tiles[j, ct][:, rows], rhs=ident[:], is_transpose=True, start=False, stop=True)
+                    o_half = xa[j][:, b, half * BANK : (half + 1) * BANK]
                     nc.vector.scalar_tensor_tensor(
-                        out=res[:], in0=o, scalar=neg_mean[:, i : i + 1], in1=ln_gain[:], op0=ALU.add, op1=ALU.mult
+                        out=o_half, in0=res_v[:], scalar=1.0, in1=o_half, op0=ALU.mult, op1=ALU.add,
+                        accum_out=row_sum[:, i, half : half + 1],
                     )
-                    nc.scalar.activation(out=res[:], in_=res[:], func=ACT.Copy, scale=ln_rstd[:, i : i + 1])
-                    nc.gpsimd.tensor_tensor(out=res[:], in0=res[:], in1=ln_bias[:], op=ALU.add)
-                    nc.sync.dma_start(out=out[j * P : (j + 1) * P, b, :], in_=res[:])
+                nc.vector.tensor_scalar(
+                    out=neg_mean[:, i : i + 1], in0=row_sum[:, i, 0:1], scalar1=row_sum[:, i, 1:2], scalar2=-1.0 / D,
+                    op0=ALU.add, op1=ALU.mult,
+                )
+
+            def centre_and_gain(j, b):
+                i = j * B + b
+                o = xa[j][:, b, :]
+                squares = junk.tile([P, D], BF16)
+                nc.scalar.activation(
+                    out=squares[:], in_=o, func=ACT.Square, bias=neg_mean[:, i : i + 1], scale=1.0, accum_out=sum_sq[:, i : i + 1]
+                )
+                nc.scalar.activation(
+                    out=ln_rstd[:, i : i + 1], in_=sum_sq[:, i : i + 1], func=ACT.Abs_reciprocal_sqrt, bias=eps[:], scale=1.0 / D
+                )
+                res = rowp.tile([P, D], F32)
+                nc.vector.scalar_tensor_tensor(
+                    out=res[:], in0=o, scalar=neg_mean[:, i : i + 1], in1=ln_gain[:], op0=ALU.add, op1=ALU.mult
+                )
+                res_tiles[i] = res
+
+            def scale_bias_store(j, b):
+                i = j * B + b
+                res = res_tiles[i]
+                nc.scalar.activation(out=res[:], in_=res[:], func=ACT.Copy, scale=ln_rstd[:, i : i + 1])
+                nc.gpsimd.tensor_tensor(out=res[:], in0=res[:], in1=ln_bias[:], op=ALU.add)
+                nc.sync.dma_start(out=out[j * P : (j + 1) * P, b, :], in_=res[:])
+
+            ahead = C_TILES // B
+            for ct in range(C_TILES):
+                batch_norm_prelu(0, ct)
+            for i in range(L_TILES * B):
+                j, b = divmod(i, B)
+                sum_of_streams(j, b)
+                if j + 1 < L_TILES:
+                    for ct in range(b * ahead, (b + 1) * ahead):
+                        batch_norm_prelu(j + 1, ct)
+                if i > 0:
+                    scale_bias_store(*divmod(i - 1, B))
+                centre_and_gain(j, b)
+            scale_bias_store(L_TILES - 1, B - 1)

@@ -17,6 +17,7 @@ PASSES = 2
 GROUP = 512
 TILES = GROUP // P
 L_TILES = L // P
+ROW_TILES = L_TILES * B
 W_GROUPS = D // GROUP
 C_TILES = D // P
 BANK = 512
@@ -38,32 +39,16 @@ def quantise_group(nc, raws, stage, psum_t, ident, rows, codes, scales):
             for u in range(2):
                 first = (2 * g + u) * P
                 nc.tensor.transpose(xt[:, g, u, :], words[:, first : first + P], ident[:])
-        nc.scalar.copy(
-            out=grouped_words[:, :, r * P : (r + 1) * P, :],
-            in_=xt[:].rearrange("p g u r -> p g r u"),
-        )
+        side_by_side = grouped_words[:, :, r * P : (r + 1) * P, :]
+        if r % 2 == 0:
+            nc.scalar.copy(out=side_by_side, in_=xt[:].rearrange("p g u r -> p g r u"))
+        else:
+            nc.vector.tensor_copy(out=side_by_side, in_=xt[:].rearrange("p g u r -> p g r u"))
     nc.vector.quantize_mx(
         out=codes.rearrange("p g r -> p (g r)").bitcast(FP8X4),
         scales=scales.rearrange("p g r -> p (g r)"),
         in_=grouped[:],
     )
-
-
-def product_tile(nc, psum_y, w_codes, w_scales, c_codes, c_scales, ct):
-    h, q = divmod(ct, TILES)
-    cols = slice(q * P, (q + 1) * P)
-    y = psum_y.tile([P, GROUP], F32, tag="y")
-    for g in range(PASSES):
-        nc.tensor.matmul_mx(
-            out=y[:],
-            lhsT=w_codes[h][:, g, cols].bitcast(FP8X4),
-            lhsT_scale=w_scales[h][:, g, cols],
-            rhs=c_codes[:, g, :].bitcast(FP8X4),
-            rhs_scale=c_scales[:, g, :],
-            start=(g == 0),
-            stop=(g == PASSES - 1),
-        )
-    return y
 
 
 def tile_coattention_pb_kernel(tc, x, res_a, ctx_v, W_v, bn_v_g, bn_v_b, prelu_v, ln_g, ln_b, out):
@@ -72,46 +57,66 @@ def tile_coattention_pb_kernel(tc, x, res_a, ctx_v, W_v, bn_v_g, bn_v_b, prelu_v
         whole.enter_context(tc.manual_schedule())
         const = whole.enter_context(tc.tile_pool(name="const", bufs=1))
         keep = whole.enter_context(tc.tile_pool(name="keep", bufs=1))
-        streams = whole.enter_context(tc.tile_pool(name="streams", bufs=2))
-        psum_y = whole.enter_context(tc.psum_pool(name="psum_y", bufs=4))
+        streams = whole.enter_context(tc.tile_pool(name="streams", bufs=3))
+        psum_g = whole.enter_context(tc.psum_pool(name="psum_g", bufs=1))
 
         ident = const.tile([P, P], F32)
         make_identity(nc, ident[:])
         ident_bf = const.tile([P, P], BF16)
         make_identity(nc, ident_bf[:])
+        ones_bf = const.tile([P, P], BF16)
+        nc.vector.memset(ones_bf[:], 1.0)
         eps = const.tile([P, 1], F32)
         nc.vector.memset(eps[:], EPS)
         table_first = const.tile([P, 1], F32)
         nc.scalar.activation(out=table_first[:], in_=eps[:], func=ACT.Abs_reciprocal_sqrt)
 
-        bn_rows = const.tile([P, P], BF16)
-        nc.vector.memset(bn_rows[:], 0.0)
-        nc.sync.dma_start(out=bn_rows[0:C_TILES, :], in_=bn_v_g.rearrange("(t c) -> t c", t=C_TILES))
-        nc.sync.dma_start(out=bn_rows[C_TILES : 2 * C_TILES, :], in_=bn_v_b.rearrange("(t c) -> t c", t=C_TILES))
         slope = const.tile([P, 1], BF16)
         nc.sync.dma_start(out=slope[:], in_=prelu_v.partition_broadcast(P))
         slope_less_1 = const.tile([P, 1], F32)
         nc.vector.tensor_scalar_add(out=slope_less_1[:], in0=slope[:], scalar1=-1.0)
 
-        w_codes = [keep.tile([P, PASSES, GROUP], U32, align_bytes=64, name="w_codes%d" % h) for h in range(W_GROUPS)]
-        w_scales = [keep.tile([P, PASSES, GROUP], U8, align_bytes=64, name="w_scales%d" % h) for h in range(W_GROUPS)]
-        c_codes = [keep.tile([P, PASSES, GROUP], U32, align_bytes=64, name="c_codes%d" % j) for j in range(L_TILES)]
-        c_scales = [keep.tile([P, PASSES, GROUP], U8, align_bytes=64, name="c_scales%d" % j) for j in range(L_TILES)]
+        bn_gain_bias = const.tile([P, 2 * C_TILES], F32)
+        ln_bias = const.tile([P, D], F32)
+        ln_gain = [psum_g.tile([P, BANK], F32, name="ln_gain%d" % half) for half in range(HALVES)]
+        y_sb = {}
         stats = keep.tile([P, C_TILES, L_TILES, 6], F32)
+        mean_var = keep.tile([P, C_TILES, 2], F32)
 
         with ExitStack() as first:
-            raws = first.enter_context(tc.tile_pool(name="raws", bufs=3))
+            mx = first.enter_context(tc.tile_pool(name="mx", bufs=1))
+            raws = first.enter_context(tc.tile_pool(name="raws", bufs=2))
             stage = first.enter_context(tc.tile_pool(name="stage", bufs=2))
-            psum_t = first.enter_context(tc.psum_pool(name="psum_t", bufs=4))
+            psum_t = first.enter_context(tc.psum_pool(name="psum_t", bufs=3))
+            psum_y = first.enter_context(tc.psum_pool(name="psum_y", bufs=3))
+
+            bn_rows = mx.tile([P, P], BF16)
+            nc.vector.memset(bn_rows[:], 0.0)
+            nc.sync.dma_start(out=bn_rows[0:C_TILES, :], in_=bn_v_g.rearrange("(t c) -> t c", t=C_TILES))
+            nc.sync.dma_start(out=bn_rows[C_TILES : 2 * C_TILES, :], in_=bn_v_b.rearrange("(t c) -> t c", t=C_TILES))
+            bn_cols = psum_t.tile([P, P], BF16, tag="xt")
+            nc.tensor.transpose(bn_cols[:], bn_rows[:], ident_bf[:])
+            nc.vector.tensor_copy(out=bn_gain_bias[:], in_=bn_cols[:, 0 : 2 * C_TILES])
+
+            ln_rows = mx.tile([P, 2 * D], BF16)
+            nc.vector.memset(ln_rows[:], 0.0)
+            nc.sync.dma_start(out=ln_rows[0:1, 0:D], in_=ln_g.rearrange("(o c) -> o c", o=1))
+            nc.sync.dma_start(out=ln_rows[0:1, D : 2 * D], in_=ln_b.rearrange("(o c) -> o c", o=1))
+            for half in range(HALVES):
+                cols = slice(half * BANK, (half + 1) * BANK)
+                nc.tensor.matmul(ln_gain[half][:], lhsT=ones_bf[:], rhs=ln_rows[:, cols], start=True, stop=True)
+                bias_ps = psum_t.tile([P, BANK], F32, tag="xt")
+                nc.tensor.matmul(bias_ps[:], lhsT=ones_bf[:], rhs=ln_rows[:, D + half * BANK : D + (half + 1) * BANK], start=True, stop=True)
+                nc.vector.tensor_copy(out=ln_bias[:, cols], in_=bias_ps[:])
+
+            w_codes = [mx.tile([P, PASSES, GROUP], U32, align_bytes=64, name="w_codes%d" % h) for h in range(W_GROUPS)]
+            w_scales = [mx.tile([P, PASSES, GROUP], U8, align_bytes=64, name="w_scales%d" % h) for h in range(W_GROUPS)]
+            c_codes = [mx.tile([P, PASSES, GROUP], U32, align_bytes=64, name="c_codes%d" % j) for j in range(L_TILES)]
+            c_scales = [mx.tile([P, PASSES, GROUP], U8, align_bytes=64, name="c_scales%d" % j) for j in range(L_TILES)]
 
             def quantise_ctx(j):
                 rows = ctx_v[:, j * P : (j + 1) * P, :].rearrange("b l k -> l b k")
                 quantise_group(nc, raws, stage, psum_t, ident, rows, c_codes[j][:], c_scales[j][:])
-
-            bn_cols = psum_t.tile([P, P], BF16, tag="xt")
-            nc.tensor.transpose(bn_cols[:], bn_rows[:], ident_bf[:])
-            bn_gain_bias = const.tile([P, 2 * C_TILES], F32)
-            nc.vector.tensor_copy(out=bn_gain_bias[:], in_=bn_cols[:, 0 : 2 * C_TILES])
 
             for h in range(W_GROUPS):
                 rows = W_v[h * GROUP : (h + 1) * GROUP, :].rearrange("(r p) k -> p r k", p=P)
@@ -121,27 +126,38 @@ def tile_coattention_pb_kernel(tc, x, res_a, ctx_v, W_v, bn_v_g, bn_v_b, prelu_v
                 if j + 1 < L_TILES:
                     quantise_ctx(j + 1)
                 for ct in range(C_TILES):
-                    y = product_tile(nc, psum_y, w_codes, w_scales, c_codes[j], c_scales[j], ct)
+                    h, q = divmod(ct, TILES)
+                    cols = slice(q * P, (q + 1) * P)
+                    y = psum_y.tile([P, GROUP], F32)
+                    for g in range(PASSES):
+                        nc.tensor.matmul_mx(
+                            out=y[:],
+                            lhsT=w_codes[h][:, g, cols].bitcast(FP8X4),
+                            lhsT_scale=w_scales[h][:, g, cols],
+                            rhs=c_codes[j][:, g, :].bitcast(FP8X4),
+                            rhs_scale=c_scales[j][:, g, :],
+                            start=(g == 0),
+                            stop=(g == PASSES - 1),
+                        )
                     nc.vector.bn_stats(out=stats[:, ct, j, :], in_=y[:])
+                    y_sb[j, ct] = keep.tile([P, GROUP], F32, name="y_sb%d_%d" % (j, ct))
+                    nc.scalar.copy(out=y_sb[j, ct][:], in_=y[:])
+                    if j == L_TILES - 1:
+                        nc.vector.bn_aggr(out=mean_var[:, ct, :], in_=stats[:, ct, :, :].rearrange("p j s -> p (j s)"))
 
         xa = []
+        pair = 2
         for j in range(L_TILES):
-            x_t = streams.tile([P, B, D], BF16)
-            nc.sync.dma_start(out=x_t[:], in_=x[j * P : (j + 1) * P, :, :])
-            a_t = streams.tile([P, B, D], BF16)
-            nc.sync.dma_start(out=a_t[:], in_=res_a[:, j * P : (j + 1) * P, :].rearrange("b l c -> l b c"))
             xa_j = keep.tile([P, B, D], F32, name="xa%d" % j)
-            for b in range(B):
-                nc.gpsimd.tensor_tensor(out=xa_j[:, b, :], in0=x_t[:, b, :], in1=a_t[:, b, :], op=ALU.add)
+            for b0 in range(0, B, pair):
+                x_t = streams.tile([P, pair, D], BF16)
+                nc.sync.dma_start(out=x_t[:], in_=x[j * P : (j + 1) * P, b0 : b0 + pair, :])
+                a_t = streams.tile([P, pair, D], BF16)
+                nc.sync.dma_start(out=a_t[:], in_=res_a[b0 : b0 + pair, j * P : (j + 1) * P, :].rearrange("b l c -> l b c"))
+                for s in range(pair):
+                    nc.gpsimd.tensor_tensor(out=xa_j[:, b0 + s, :], in0=x_t[:, s, :], in1=a_t[:, s, :], op=ALU.add)
             xa.append(xa_j)
-        ln_gain = const.tile([P, D], BF16)
-        nc.sync.dma_start(out=ln_gain[:], in_=ln_g.partition_broadcast(P))
-        ln_bias = const.tile([P, D], BF16)
-        nc.sync.dma_start(out=ln_bias[:], in_=ln_b.partition_broadcast(P))
 
-        mean_var = keep.tile([P, C_TILES, 2], F32)
-        for ct in range(C_TILES):
-            nc.vector.bn_aggr(out=mean_var[:, ct, :], in_=stats[:, ct, :, :].rearrange("p j s -> p (j s)"))
         bn_rstd = keep.tile([P, C_TILES], F32)
         nc.scalar.activation(out=bn_rstd[:], in_=mean_var[:, :, 1], func=ACT.Abs_reciprocal_sqrt, bias=eps[:], scale=1.0)
         bn_scale = keep.tile([P, C_TILES], F32)
@@ -150,29 +166,32 @@ def tile_coattention_pb_kernel(tc, x, res_a, ctx_v, W_v, bn_v_g, bn_v_b, prelu_v
         nc.vector.tensor_mul(out=bn_shift[:], in0=mean_var[:, :, 0], in1=bn_scale[:])
         nc.vector.tensor_sub(out=bn_shift[:], in0=bn_gain_bias[:, C_TILES : 2 * C_TILES], in1=bn_shift[:])
 
-        row_sum = keep.tile([P, L_TILES * B, HALVES], F32)
-        neg_mean = keep.tile([P, L_TILES * B], F32)
-        sum_sq = keep.tile([P, L_TILES * B], F32)
-        ln_rstd = keep.tile([P, L_TILES * B], F32)
+        row_sum = keep.tile([P, ROW_TILES, HALVES], F32)
+        neg_mean = keep.tile([P, ROW_TILES], F32)
+        sum_sq = keep.tile([P, ROW_TILES], F32)
+        ln_rstd = keep.tile([P, ROW_TILES], F32)
         with ExitStack() as second:
             chan = second.enter_context(tc.tile_pool(name="chan", bufs=2 * C_TILES))
             junk = second.enter_context(tc.tile_pool(name="junk", bufs=2))
             rowp = second.enter_context(tc.tile_pool(name="rowp", bufs=5))
-            psum_o = second.enter_context(tc.psum_pool(name="psum_o", bufs=4))
-            z_tiles = {}
+            psum_o = second.enter_context(tc.psum_pool(name="psum_o", bufs=6))
             n_tiles = {}
             res_tiles = {}
 
             def batch_norm_prelu(j, ct):
-                y = product_tile(nc, psum_y, w_codes, w_scales, c_codes[j], c_scales[j], ct)
-                z = chan.tile([P, GROUP], F32)
+                z0 = y_sb[j, ct]
+                z1 = y_sb[j, ct + 1]
                 nc.scalar.activation(
-                    out=z[:], in_=y[:], func=ACT.Identity, bias=bn_shift[:, ct : ct + 1], scale=bn_scale[:, ct : ct + 1]
+                    out=z0[:], in_=z0[:], func=ACT.Identity, bias=bn_shift[:, ct : ct + 1], scale=bn_scale[:, ct : ct + 1]
                 )
-                n = chan.tile([P, GROUP], F32)
-                nc.vector.tensor_scalar(out=n[:], in0=z[:], scalar1=0.0, scalar2=slope_less_1[:], op0=ALU.min, op1=ALU.mult)
-                z_tiles[j, ct] = z
-                n_tiles[j, ct] = n
+                nc.vector.tensor_scalar(
+                    out=z1[:], in0=z1[:], scalar1=bn_scale[:, ct + 1 : ct + 2], scalar2=bn_shift[:, ct + 1 : ct + 2],
+                    op0=ALU.mult, op1=ALU.add,
+                )
+                for c, z in ((ct, z0), (ct + 1, z1)):
+                    n = chan.tile([P, GROUP], F32)
+                    nc.vector.tensor_scalar(out=n[:], in0=z[:], scalar1=0.0, scalar2=slope_less_1[:], op0=ALU.min, op1=ALU.mult)
+                    n_tiles[j, c] = n
 
             def sum_of_streams(j, b):
                 i = j * B + b
@@ -182,7 +201,7 @@ def tile_coattention_pb_kernel(tc, x, res_a, ctx_v, W_v, bn_v_g, bn_v_b, prelu_v
                     for q in range(TILES):
                         ct = half * TILES + q
                         cells = res_v[:, q * P : (q + 1) * P]
-                        nc.tensor.matmul(cells, lhsT=z_tiles[j, ct][:, rows], rhs=ident[:], is_transpose=True, start=True, stop=False)
+                        nc.tensor.matmul(cells, lhsT=y_sb[j, ct][:, rows], rhs=ident[:], is_transpose=True, start=True, stop=False)
                         nc.tensor.matmul(cells, lhsT=n_tiles[j, ct][:, rows], rhs=ident[:], is_transpose=True, start=False, stop=True)
                     o_half = xa[j][:, b, half * BANK : (half + 1) * BANK]
                     nc.vector.scalar_tensor_tensor(
@@ -205,9 +224,11 @@ def tile_coattention_pb_kernel(tc, x, res_a, ctx_v, W_v, bn_v_g, bn_v_b, prelu_v
                     out=ln_rstd[:, i : i + 1], in_=sum_sq[:, i : i + 1], func=ACT.Abs_reciprocal_sqrt, bias=eps[:], scale=1.0 / D
                 )
                 res = rowp.tile([P, D], F32)
-                nc.vector.scalar_tensor_tensor(
-                    out=res[:], in0=o, scalar=neg_mean[:, i : i + 1], in1=ln_gain[:], op0=ALU.add, op1=ALU.mult
-                )
+                for half in range(HALVES):
+                    cols = slice(half * BANK, (half + 1) * BANK)
+                    nc.vector.scalar_tensor_tensor(
+                        out=res[:, cols], in0=o[:, cols], scalar=neg_mean[:, i : i + 1], in1=ln_gain[half][:], op0=ALU.add, op1=ALU.mult
+                    )
                 res_tiles[i] = res
 
             def scale_bias_store(j, b):
@@ -217,15 +238,13 @@ def tile_coattention_pb_kernel(tc, x, res_a, ctx_v, W_v, bn_v_g, bn_v_b, prelu_v
                 nc.gpsimd.tensor_tensor(out=res[:], in0=res[:], in1=ln_bias[:], op=ALU.add)
                 nc.sync.dma_start(out=out[j * P : (j + 1) * P, b, :], in_=res[:])
 
-            ahead = C_TILES // B
-            for ct in range(C_TILES):
+            for ct in range(0, C_TILES, 2):
                 batch_norm_prelu(0, ct)
-            for i in range(L_TILES * B):
+            for i in range(ROW_TILES):
                 j, b = divmod(i, B)
                 sum_of_streams(j, b)
                 if j + 1 < L_TILES:
-                    for ct in range(b * ahead, (b + 1) * ahead):
-                        batch_norm_prelu(j + 1, ct)
+                    batch_norm_prelu(j + 1, 2 * b)
                 if i > 0:
                     scale_bias_store(*divmod(i - 1, B))
                 centre_and_gain(j, b)

@@ -22,14 +22,13 @@ W_GROUPS = D // GROUP
 C_TILES = D // P
 BANK = 512
 HALVES = D // BANK
+DEPTH = 3
 EPS = 1e-5
 
 FLOPS = 2 * L * B * D * D
 
 
-def quantise_group(nc, raws, stage, psum_t, ident, rows, codes, scales):
-    raw = raws.tile([P, TILES, D], BF16)
-    nc.sync.dma_start(out=raw[:], in_=rows)
+def transpose_group(nc, stage, psum_t, ident, raw):
     grouped = stage.tile([P, PASSES * GROUP * 4], BF16, align_bytes=64)
     grouped_words = grouped[:].bitcast(F32).rearrange("p (g r u) -> p g r u", g=PASSES, u=2)
     for r in range(TILES):
@@ -44,11 +43,18 @@ def quantise_group(nc, raws, stage, psum_t, ident, rows, codes, scales):
             nc.scalar.copy(out=side_by_side, in_=xt[:].rearrange("p g u r -> p g r u"))
         else:
             nc.vector.tensor_copy(out=side_by_side, in_=xt[:].rearrange("p g u r -> p g r u"))
+    return grouped
+
+
+def quantise(nc, pool, grouped):
+    codes = pool.tile([P, PASSES, GROUP], U32, align_bytes=64)
+    scales = pool.tile([P, PASSES, GROUP], U8, align_bytes=64)
     nc.vector.quantize_mx(
-        out=codes.rearrange("p g r -> p (g r)").bitcast(FP8X4),
-        scales=scales.rearrange("p g r -> p (g r)"),
+        out=codes[:].rearrange("p g r -> p (g r)").bitcast(FP8X4),
+        scales=scales[:].rearrange("p g r -> p (g r)"),
         in_=grouped[:],
     )
+    return codes, scales
 
 
 def tile_coattention_pb_kernel(tc, x, res_a, ctx_v, W_v, bn_v_g, bn_v_b, prelu_v, ln_g, ln_b, out):
@@ -57,7 +63,7 @@ def tile_coattention_pb_kernel(tc, x, res_a, ctx_v, W_v, bn_v_g, bn_v_b, prelu_v
         whole.enter_context(tc.manual_schedule())
         const = whole.enter_context(tc.tile_pool(name="const", bufs=1))
         keep = whole.enter_context(tc.tile_pool(name="keep", bufs=1))
-        streams = whole.enter_context(tc.tile_pool(name="streams", bufs=3))
+        streams = whole.enter_context(tc.tile_pool(name="streams", bufs=2 * B))
         psum_g = whole.enter_context(tc.psum_pool(name="psum_g", bufs=1))
 
         ident = const.tile([P, P], F32)
@@ -83,9 +89,13 @@ def tile_coattention_pb_kernel(tc, x, res_a, ctx_v, W_v, bn_v_g, bn_v_b, prelu_v
         stats = keep.tile([P, C_TILES, L_TILES, 6], F32)
         mean_var = keep.tile([P, C_TILES, 2], F32)
 
+        xa = [keep.tile([P, B, D], F32, name="xa%d" % j) for j in range(L_TILES)]
+
         with ExitStack() as first:
             mx = first.enter_context(tc.tile_pool(name="mx", bufs=1))
-            raws = first.enter_context(tc.tile_pool(name="raws", bufs=2))
+            w_pool = first.enter_context(tc.tile_pool(name="w_pool", bufs=W_GROUPS))
+            c_pool = first.enter_context(tc.tile_pool(name="c_pool", bufs=2))
+            raws = first.enter_context(tc.tile_pool(name="raws", bufs=DEPTH))
             stage = first.enter_context(tc.tile_pool(name="stage", bufs=2))
             psum_t = first.enter_context(tc.psum_pool(name="psum_t", bufs=3))
             psum_y = first.enter_context(tc.psum_pool(name="psum_y", bufs=3))
@@ -98,7 +108,7 @@ def tile_coattention_pb_kernel(tc, x, res_a, ctx_v, W_v, bn_v_g, bn_v_b, prelu_v
             nc.tensor.transpose(bn_cols[:], bn_rows[:], ident_bf[:])
             nc.vector.tensor_copy(out=bn_gain_bias[:], in_=bn_cols[:, 0 : 2 * C_TILES])
 
-            ln_rows = mx.tile([P, 2 * D], BF16)
+            ln_rows = raws.tile([P, 2 * D], BF16, tag="raw")
             nc.vector.memset(ln_rows[:], 0.0)
             nc.sync.dma_start(out=ln_rows[0:1, 0:D], in_=ln_g.rearrange("(o c) -> o c", o=1))
             nc.sync.dma_start(out=ln_rows[0:1, D : 2 * D], in_=ln_b.rearrange("(o c) -> o c", o=1))
@@ -109,54 +119,58 @@ def tile_coattention_pb_kernel(tc, x, res_a, ctx_v, W_v, bn_v_g, bn_v_b, prelu_v
                 nc.tensor.matmul(bias_ps[:], lhsT=ones_bf[:], rhs=ln_rows[:, D + half * BANK : D + (half + 1) * BANK], start=True, stop=True)
                 nc.vector.tensor_copy(out=ln_bias[:, cols], in_=bias_ps[:])
 
-            w_codes = [mx.tile([P, PASSES, GROUP], U32, align_bytes=64, name="w_codes%d" % h) for h in range(W_GROUPS)]
-            w_scales = [mx.tile([P, PASSES, GROUP], U8, align_bytes=64, name="w_scales%d" % h) for h in range(W_GROUPS)]
-            c_codes = [mx.tile([P, PASSES, GROUP], U32, align_bytes=64, name="c_codes%d" % j) for j in range(L_TILES)]
-            c_scales = [mx.tile([P, PASSES, GROUP], U8, align_bytes=64, name="c_scales%d" % j) for j in range(L_TILES)]
+            sources = [W_v[h * GROUP : (h + 1) * GROUP, :].rearrange("(r p) k -> p r k", p=P) for h in range(W_GROUPS)]
+            sources += [ctx_v[:, j * P : (j + 1) * P, :].rearrange("b l k -> l b k") for j in range(L_TILES)]
+            raw_tiles = {}
 
-            def quantise_ctx(j):
-                rows = ctx_v[:, j * P : (j + 1) * P, :].rearrange("b l k -> l b k")
-                quantise_group(nc, raws, stage, psum_t, ident, rows, c_codes[j][:], c_scales[j][:])
+            def load_group(s):
+                raw = raws.tile([P, TILES, D], BF16)
+                nc.sync.dma_start(out=raw[:], in_=sources[s])
+                raw_tiles[s] = raw
 
-            for h in range(W_GROUPS):
-                rows = W_v[h * GROUP : (h + 1) * GROUP, :].rearrange("(r p) k -> p r k", p=P)
-                quantise_group(nc, raws, stage, psum_t, ident, rows, w_codes[h][:], w_scales[h][:])
-            quantise_ctx(0)
+            def prepare_group(s, pool):
+                grouped = transpose_group(nc, stage, psum_t, ident, raw_tiles[s])
+                if s + DEPTH < len(sources):
+                    load_group(s + DEPTH)
+                return quantise(nc, pool, grouped)
+
+            for s in range(DEPTH):
+                load_group(s)
+            w_mx = [prepare_group(h, w_pool) for h in range(W_GROUPS)]
+            c_mx = prepare_group(W_GROUPS, c_pool)
+
             for j in range(L_TILES):
+                for b in range(B):
+                    x_t = streams.tile([P, D], BF16)
+                    nc.sync.dma_start(out=x_t[:], in_=x[j * P : (j + 1) * P, b, :])
+                    a_t = streams.tile([P, D], BF16)
+                    nc.sync.dma_start(out=a_t[:], in_=res_a[b, j * P : (j + 1) * P, :])
+                    nc.gpsimd.tensor_tensor(out=xa[j][:, b, :], in0=x_t[:], in1=a_t[:], op=ALU.add)
+
+            for j in range(L_TILES):
+                c_codes, c_scales = c_mx
                 if j + 1 < L_TILES:
-                    quantise_ctx(j + 1)
+                    c_mx = prepare_group(W_GROUPS + j + 1, c_pool)
                 for ct in range(C_TILES):
                     h, q = divmod(ct, TILES)
+                    w_codes, w_scales = w_mx[h]
                     cols = slice(q * P, (q + 1) * P)
                     y = psum_y.tile([P, GROUP], F32)
                     for g in range(PASSES):
                         nc.tensor.matmul_mx(
                             out=y[:],
-                            lhsT=w_codes[h][:, g, cols].bitcast(FP8X4),
-                            lhsT_scale=w_scales[h][:, g, cols],
-                            rhs=c_codes[j][:, g, :].bitcast(FP8X4),
-                            rhs_scale=c_scales[j][:, g, :],
+                            lhsT=w_codes[:, g, cols].bitcast(FP8X4),
+                            lhsT_scale=w_scales[:, g, cols],
+                            rhs=c_codes[:, g, :].bitcast(FP8X4),
+                            rhs_scale=c_scales[:, g, :],
                             start=(g == 0),
                             stop=(g == PASSES - 1),
                         )
-                    nc.vector.bn_stats(out=stats[:, ct, j, :], in_=y[:])
                     y_sb[j, ct] = keep.tile([P, GROUP], F32, name="y_sb%d_%d" % (j, ct))
                     nc.scalar.copy(out=y_sb[j, ct][:], in_=y[:])
+                    nc.vector.bn_stats(out=stats[:, ct, j, :], in_=y_sb[j, ct][:])
                     if j == L_TILES - 1:
                         nc.vector.bn_aggr(out=mean_var[:, ct, :], in_=stats[:, ct, :, :].rearrange("p j s -> p (j s)"))
-
-        xa = []
-        pair = 2
-        for j in range(L_TILES):
-            xa_j = keep.tile([P, B, D], F32, name="xa%d" % j)
-            for b0 in range(0, B, pair):
-                x_t = streams.tile([P, pair, D], BF16)
-                nc.sync.dma_start(out=x_t[:], in_=x[j * P : (j + 1) * P, b0 : b0 + pair, :])
-                a_t = streams.tile([P, pair, D], BF16)
-                nc.sync.dma_start(out=a_t[:], in_=res_a[b0 : b0 + pair, j * P : (j + 1) * P, :].rearrange("b l c -> l b c"))
-                for s in range(pair):
-                    nc.gpsimd.tensor_tensor(out=xa_j[:, b0 + s, :], in0=x_t[:, s, :], in1=a_t[:, s, :], op=ALU.add)
-            xa.append(xa_j)
 
         bn_rstd = keep.tile([P, C_TILES], F32)
         nc.scalar.activation(out=bn_rstd[:], in_=mean_var[:, :, 1], func=ACT.Abs_reciprocal_sqrt, bias=eps[:], scale=1.0)

@@ -22,39 +22,13 @@ W_GROUPS = D // GROUP
 C_TILES = D // P
 BANK = 512
 HALVES = D // BANK
-DEPTH = 3
 EPS = 1e-5
+DEPTH = 3
+STREAMS = 5
+GP_SUMS = 6
+O_BUFS = 6
 
 FLOPS = 2 * L * B * D * D
-
-
-def transpose_group(nc, stage, psum_t, ident, raw):
-    grouped = stage.tile([P, PASSES * GROUP * 4], BF16, align_bytes=64)
-    grouped_words = grouped[:].bitcast(F32).rearrange("p (g r u) -> p g r u", g=PASSES, u=2)
-    for r in range(TILES):
-        words = raw[:, r, :].bitcast(F32)
-        xt = psum_t.tile([P, PASSES, 2, P], F32, tag="xt")
-        for g in range(PASSES):
-            for u in range(2):
-                first = (2 * g + u) * P
-                nc.tensor.transpose(xt[:, g, u, :], words[:, first : first + P], ident[:])
-        side_by_side = grouped_words[:, :, r * P : (r + 1) * P, :]
-        if r % 2 == 0:
-            nc.scalar.copy(out=side_by_side, in_=xt[:].rearrange("p g u r -> p g r u"))
-        else:
-            nc.vector.tensor_copy(out=side_by_side, in_=xt[:].rearrange("p g u r -> p g r u"))
-    return grouped
-
-
-def quantise(nc, pool, grouped):
-    codes = pool.tile([P, PASSES, GROUP], U32, align_bytes=64)
-    scales = pool.tile([P, PASSES, GROUP], U8, align_bytes=64)
-    nc.vector.quantize_mx(
-        out=codes[:].rearrange("p g r -> p (g r)").bitcast(FP8X4),
-        scales=scales[:].rearrange("p g r -> p (g r)"),
-        in_=grouped[:],
-    )
-    return codes, scales
 
 
 def tile_coattention_pb_kernel(tc, x, res_a, ctx_v, W_v, bn_v_g, bn_v_b, prelu_v, ln_g, ln_b, out):
@@ -62,9 +36,27 @@ def tile_coattention_pb_kernel(tc, x, res_a, ctx_v, W_v, bn_v_g, bn_v_b, prelu_v
     with ExitStack() as whole:
         whole.enter_context(tc.manual_schedule())
         const = whole.enter_context(tc.tile_pool(name="const", bufs=1))
-        keep = whole.enter_context(tc.tile_pool(name="keep", bufs=1))
-        streams = whole.enter_context(tc.tile_pool(name="streams", bufs=2 * B))
-        psum_g = whole.enter_context(tc.psum_pool(name="psum_g", bufs=1))
+        slabs = whole.enter_context(tc.tile_pool(name="slabs", bufs=L_TILES * C_TILES + 1))
+        streams = whole.enter_context(tc.tile_pool(name="streams", bufs=STREAMS))
+        rows_pool = whole.enter_context(tc.tile_pool(name="rows_pool", bufs=O_BUFS))
+        res_pool = whole.enter_context(tc.tile_pool(name="res_pool", bufs=4))
+        junk_pool = whole.enter_context(tc.tile_pool(name="junk_pool", bufs=2))
+        mx = whole.enter_context(tc.tile_pool(name="mx", bufs=1))
+        psum = whole.enter_context(tc.psum_pool(name="psum", bufs=8))
+
+        w_rows = [W_v[h * GROUP : (h + 1) * GROUP, :].rearrange("(r p) k -> p r k", p=P) for h in range(W_GROUPS)]
+        c_rows = [ctx_v[:, j * P : (j + 1) * P, :].rearrange("b l k -> l b k") for j in range(L_TILES)]
+        sources = [w_rows[0]] + c_rows + [w_rows[1]]
+        raw_tiles = {}
+
+        def load_group(s):
+            for hf in range(2):
+                raw = slabs.tile([P, 2, D], BF16, tag="slab", name="raw", align_bytes=64)
+                nc.sync.dma_start(out=raw[:], in_=sources[s][:, 2 * hf : 2 * hf + 2, :])
+                raw_tiles[s, hf] = raw
+
+        for s in range(DEPTH):
+            load_group(s)
 
         ident = const.tile([P, P], F32)
         make_identity(nc, ident[:])
@@ -77,189 +69,295 @@ def tile_coattention_pb_kernel(tc, x, res_a, ctx_v, W_v, bn_v_g, bn_v_b, prelu_v
         table_first = const.tile([P, 1], F32)
         nc.scalar.activation(out=table_first[:], in_=eps[:], func=ACT.Abs_reciprocal_sqrt)
 
+        bn_rows = const.tile([P, P], BF16)
+        nc.vector.memset(bn_rows[:], 0.0)
+        ln_rows = const.tile([P, 2 * D], BF16)
+        nc.vector.memset(ln_rows[:], 0.0)
         slope = const.tile([P, 1], BF16)
-        nc.sync.dma_start(out=slope[:], in_=prelu_v.partition_broadcast(P))
+        nc.scalar.dma_start(out=slope[:], in_=prelu_v.partition_broadcast(P))
+        nc.scalar.dma_start(out=bn_rows[0:C_TILES, :], in_=bn_v_g.rearrange("(t c) -> t c", t=C_TILES))
+        nc.scalar.dma_start(out=bn_rows[C_TILES : 2 * C_TILES, :], in_=bn_v_b.rearrange("(t c) -> t c", t=C_TILES))
+        nc.scalar.dma_start(out=ln_rows[0:1, 0:D], in_=ln_g.rearrange("(o c) -> o c", o=1))
+        nc.scalar.dma_start(out=ln_rows[0:1, D : 2 * D], in_=ln_b.rearrange("(o c) -> o c", o=1))
+
         slope_less_1 = const.tile([P, 1], F32)
-        nc.vector.tensor_scalar_add(out=slope_less_1[:], in0=slope[:], scalar1=-1.0)
-
         bn_gain_bias = const.tile([P, 2 * C_TILES], F32)
+        neg_gain = const.tile([P, C_TILES], F32)
         ln_bias = const.tile([P, D], F32)
-        ln_gain = [psum_g.tile([P, BANK], F32, name="ln_gain%d" % half) for half in range(HALVES)]
-        y_sb = {}
-        stats = keep.tile([P, C_TILES, L_TILES, 6], F32)
-        mean_var = keep.tile([P, C_TILES, 2], F32)
+        stats = const.tile([P, C_TILES, L_TILES, 6], F32)
+        mean_var = const.tile([P, C_TILES, 2], F32)
+        bn_rstd = const.tile([P, C_TILES], F32)
+        bn_scale = const.tile([P, C_TILES], F32)
+        bn_neg_scale = const.tile([P, C_TILES], F32)
+        bn_shift = const.tile([P, C_TILES], F32)
+        row_sum = const.tile([P, ROW_TILES, HALVES], F32)
+        neg_mean = const.tile([P, ROW_TILES], F32)
+        sum_sq = const.tile([P, ROW_TILES], F32)
+        ln_rstd = const.tile([P, ROW_TILES], F32)
 
-        xa = [keep.tile([P, B, D], F32, name="xa%d" % j) for j in range(L_TILES)]
+        def bank(name):
+            tile = psum.tile([P, BANK], F32, tag="bank", name=name)
+            return tile
 
-        with ExitStack() as first:
-            mx = first.enter_context(tc.tile_pool(name="mx", bufs=1))
-            w_pool = first.enter_context(tc.tile_pool(name="w_pool", bufs=W_GROUPS))
-            c_pool = first.enter_context(tc.tile_pool(name="c_pool", bufs=2))
-            raws = first.enter_context(tc.tile_pool(name="raws", bufs=DEPTH))
-            stage = first.enter_context(tc.tile_pool(name="stage", bufs=2))
-            psum_t = first.enter_context(tc.psum_pool(name="psum_t", bufs=3))
-            psum_y = first.enter_context(tc.psum_pool(name="psum_y", bufs=3))
+        mx_tiles = {}
 
-            bn_rows = mx.tile([P, P], BF16)
-            nc.vector.memset(bn_rows[:], 0.0)
-            nc.sync.dma_start(out=bn_rows[0:C_TILES, :], in_=bn_v_g.rearrange("(t c) -> t c", t=C_TILES))
-            nc.sync.dma_start(out=bn_rows[C_TILES : 2 * C_TILES, :], in_=bn_v_b.rearrange("(t c) -> t c", t=C_TILES))
-            bn_cols = psum_t.tile([P, P], BF16, tag="xt")
-            nc.tensor.transpose(bn_cols[:], bn_rows[:], ident_bf[:])
-            nc.vector.tensor_copy(out=bn_gain_bias[:], in_=bn_cols[:, 0 : 2 * C_TILES])
+        def prepare_group(s):
+            codes = mx.tile([P, PASSES, GROUP], U32, name="codes%d" % s, align_bytes=64)
+            scales = mx.tile([P, PASSES, GROUP], U8, name="scales%d" % s, align_bytes=64)
+            staged = []
+            for g in range(PASSES):
+                grouped = slabs.tile([P, GROUP * 4], BF16, tag="slab", name="grouped", align_bytes=64)
+                staged.append(grouped)
+                words_out = grouped[:].bitcast(F32).rearrange("p (q r u) -> p q r u", q=2, u=2)
+                for hf in range(2):
+                    xt = bank("xt")
+                    planes = xt[:].rearrange("p (t u r) -> p t u r", t=2, u=2)
+                    for t in range(2):
+                        words = raw_tiles[s, hf][:, t, :].bitcast(F32)
+                        for u in range(2):
+                            first = (2 * g + u) * P
+                            nc.tensor.transpose(planes[:, t, u, :], words[:, first : first + P], ident[:])
+                    src = planes.rearrange("p t u r -> p t r u")
+                    dst = words_out[:, hf, :, :].rearrange("p (t r) u -> p t r u", t=2)
+                    if g == PASSES - 1 and hf == 1:
+                        nc.vector.tensor_copy(out=dst, in_=src)
+                    else:
+                        nc.scalar.copy(out=dst, in_=src)
+            if s + DEPTH < len(sources):
+                load_group(s + DEPTH)
+            for g in range(PASSES):
+                nc.vector.quantize_mx(out=codes[:, g, :].bitcast(FP8X4), scales=scales[:, g, :], in_=staged[g][:])
+            mx_tiles[s] = (codes, scales)
 
-            ln_rows = raws.tile([P, 2 * D], BF16, tag="raw")
-            nc.vector.memset(ln_rows[:], 0.0)
-            nc.sync.dma_start(out=ln_rows[0:1, 0:D], in_=ln_g.rearrange("(o c) -> o c", o=1))
-            nc.sync.dma_start(out=ln_rows[0:1, D : 2 * D], in_=ln_b.rearrange("(o c) -> o c", o=1))
-            for half in range(HALVES):
-                cols = slice(half * BANK, (half + 1) * BANK)
-                nc.tensor.matmul(ln_gain[half][:], lhsT=ones_bf[:], rhs=ln_rows[:, cols], start=True, stop=True)
-                bias_ps = psum_t.tile([P, BANK], F32, tag="xt")
-                nc.tensor.matmul(bias_ps[:], lhsT=ones_bf[:], rhs=ln_rows[:, D + half * BANK : D + (half + 1) * BANK], start=True, stop=True)
-                nc.vector.tensor_copy(out=ln_bias[:, cols], in_=bias_ps[:])
+        y_tiles = {}
+        zn = {}
 
-            sources = [W_v[h * GROUP : (h + 1) * GROUP, :].rearrange("(r p) k -> p r k", p=P) for h in range(W_GROUPS)]
-            sources += [ctx_v[:, j * P : (j + 1) * P, :].rearrange("b l k -> l b k") for j in range(L_TILES)]
-            raw_tiles = {}
+        def product(ct, j):
+            h, q = divmod(ct, TILES)
+            w_codes, w_scales = mx_tiles[0 if h == 0 else L_TILES + 1]
+            c_codes, c_scales = mx_tiles[1 + j]
+            cols = slice(q * P, (q + 1) * P)
+            y = bank("y")
+            for g in range(PASSES):
+                nc.tensor.matmul_mx(
+                    out=y[:],
+                    lhsT=w_codes[:, g, cols].bitcast(FP8X4),
+                    lhsT_scale=w_scales[:, g, cols],
+                    rhs=c_codes[:, g, :].bitcast(FP8X4),
+                    rhs_scale=c_scales[:, g, :],
+                    start=(g == 0),
+                    stop=(g == PASSES - 1),
+                )
+            y_tiles[ct, j] = y
 
-            def load_group(s):
-                raw = raws.tile([P, TILES, D], BF16)
-                nc.sync.dma_start(out=raw[:], in_=sources[s])
-                raw_tiles[s] = raw
+        def statistics(ct, j):
+            nc.vector.bn_stats(out=stats[:, ct, j, :], in_=y_tiles[ct, j][:])
+            if j == L_TILES - 1:
+                nc.vector.bn_aggr(out=mean_var[:, ct, :], in_=stats[:, ct, :, :].rearrange("p j s -> p (j s)"))
 
-            def prepare_group(s, pool):
-                grouped = transpose_group(nc, stage, psum_t, ident, raw_tiles[s])
-                if s + DEPTH < len(sources):
-                    load_group(s + DEPTH)
-                return quantise(nc, pool, grouped)
+        def col(tile, ct):
+            return tile[:, ct : ct + 1]
 
-            for s in range(DEPTH):
-                load_group(s)
-            w_mx = [prepare_group(h, w_pool) for h in range(W_GROUPS)]
-            c_mx = prepare_group(W_GROUPS, c_pool)
-
-            for j in range(L_TILES):
-                for b in range(B):
-                    x_t = streams.tile([P, D], BF16)
-                    nc.sync.dma_start(out=x_t[:], in_=x[j * P : (j + 1) * P, b, :])
-                    a_t = streams.tile([P, D], BF16)
-                    nc.sync.dma_start(out=a_t[:], in_=res_a[b, j * P : (j + 1) * P, :])
-                    nc.gpsimd.tensor_tensor(out=xa[j][:, b, :], in0=x_t[:], in1=a_t[:], op=ALU.add)
-
-            for j in range(L_TILES):
-                c_codes, c_scales = c_mx
-                if j + 1 < L_TILES:
-                    c_mx = prepare_group(W_GROUPS + j + 1, c_pool)
-                for ct in range(C_TILES):
-                    h, q = divmod(ct, TILES)
-                    w_codes, w_scales = w_mx[h]
-                    cols = slice(q * P, (q + 1) * P)
-                    y = psum_y.tile([P, GROUP], F32)
-                    for g in range(PASSES):
-                        nc.tensor.matmul_mx(
-                            out=y[:],
-                            lhsT=w_codes[:, g, cols].bitcast(FP8X4),
-                            lhsT_scale=w_scales[:, g, cols],
-                            rhs=c_codes[:, g, :].bitcast(FP8X4),
-                            rhs_scale=c_scales[:, g, :],
-                            start=(g == 0),
-                            stop=(g == PASSES - 1),
-                        )
-                    y_sb[j, ct] = keep.tile([P, GROUP], F32, name="y_sb%d_%d" % (j, ct))
-                    nc.scalar.copy(out=y_sb[j, ct][:], in_=y[:])
-                    nc.vector.bn_stats(out=stats[:, ct, j, :], in_=y_sb[j, ct][:])
-                    if j == L_TILES - 1:
-                        nc.vector.bn_aggr(out=mean_var[:, ct, :], in_=stats[:, ct, :, :].rearrange("p j s -> p (j s)"))
-
-        bn_rstd = keep.tile([P, C_TILES], F32)
-        nc.scalar.activation(out=bn_rstd[:], in_=mean_var[:, :, 1], func=ACT.Abs_reciprocal_sqrt, bias=eps[:], scale=1.0)
-        bn_scale = keep.tile([P, C_TILES], F32)
-        nc.vector.tensor_mul(out=bn_scale[:], in0=bn_rstd[:], in1=bn_gain_bias[:, 0:C_TILES])
-        bn_shift = keep.tile([P, C_TILES], F32)
-        nc.vector.tensor_mul(out=bn_shift[:], in0=mean_var[:, :, 0], in1=bn_scale[:])
-        nc.vector.tensor_sub(out=bn_shift[:], in0=bn_gain_bias[:, C_TILES : 2 * C_TILES], in1=bn_shift[:])
-
-        row_sum = keep.tile([P, ROW_TILES, HALVES], F32)
-        neg_mean = keep.tile([P, ROW_TILES], F32)
-        sum_sq = keep.tile([P, ROW_TILES], F32)
-        ln_rstd = keep.tile([P, ROW_TILES], F32)
-        with ExitStack() as second:
-            chan = second.enter_context(tc.tile_pool(name="chan", bufs=2 * C_TILES))
-            junk = second.enter_context(tc.tile_pool(name="junk", bufs=2))
-            rowp = second.enter_context(tc.tile_pool(name="rowp", bufs=5))
-            psum_o = second.enter_context(tc.psum_pool(name="psum_o", bufs=6))
-            n_tiles = {}
-            res_tiles = {}
-
-            def batch_norm_prelu(j, ct):
-                z0 = y_sb[j, ct]
-                z1 = y_sb[j, ct + 1]
+        def bn_prepare(ct, step):
+            if step == 0:
                 nc.scalar.activation(
-                    out=z0[:], in_=z0[:], func=ACT.Identity, bias=bn_shift[:, ct : ct + 1], scale=bn_scale[:, ct : ct + 1]
+                    out=col(bn_rstd, ct), in_=mean_var[:, ct, 1:2], func=ACT.Abs_reciprocal_sqrt, bias=eps[:], scale=1.0
                 )
-                nc.vector.tensor_scalar(
-                    out=z1[:], in0=z1[:], scalar1=bn_scale[:, ct + 1 : ct + 2], scalar2=bn_shift[:, ct + 1 : ct + 2],
-                    op0=ALU.mult, op1=ALU.add,
-                )
-                for c, z in ((ct, z0), (ct + 1, z1)):
-                    n = chan.tile([P, GROUP], F32)
-                    nc.vector.tensor_scalar(out=n[:], in0=z[:], scalar1=0.0, scalar2=slope_less_1[:], op0=ALU.min, op1=ALU.mult)
-                    n_tiles[j, c] = n
-
-            def sum_of_streams(j, b):
-                i = j * B + b
-                rows = slice(b * P, (b + 1) * P)
-                for half in range(HALVES):
-                    res_v = psum_o.tile([P, BANK], F32)
-                    for q in range(TILES):
-                        ct = half * TILES + q
-                        cells = res_v[:, q * P : (q + 1) * P]
-                        nc.tensor.matmul(cells, lhsT=y_sb[j, ct][:, rows], rhs=ident[:], is_transpose=True, start=True, stop=False)
-                        nc.tensor.matmul(cells, lhsT=n_tiles[j, ct][:, rows], rhs=ident[:], is_transpose=True, start=False, stop=True)
-                    o_half = xa[j][:, b, half * BANK : (half + 1) * BANK]
-                    nc.vector.scalar_tensor_tensor(
-                        out=o_half, in0=res_v[:], scalar=1.0, in1=o_half, op0=ALU.mult, op1=ALU.add,
-                        accum_out=row_sum[:, i, half : half + 1],
-                    )
-                nc.vector.tensor_scalar(
-                    out=neg_mean[:, i : i + 1], in0=row_sum[:, i, 0:1], scalar1=row_sum[:, i, 1:2], scalar2=-1.0 / D,
-                    op0=ALU.add, op1=ALU.mult,
+            elif step == 1:
+                nc.scalar.activation(out=col(bn_neg_scale, ct), in_=col(bn_rstd, ct), func=ACT.Copy, scale=col(neg_gain, ct))
+                nc.scalar.activation(out=col(bn_scale, ct), in_=col(bn_rstd, ct), func=ACT.Copy, scale=col(bn_gain_bias, ct))
+            else:
+                nc.scalar.activation(
+                    out=col(bn_shift, ct), in_=mean_var[:, ct, 0:1], func=ACT.Identity,
+                    bias=col(bn_gain_bias, C_TILES + ct), scale=col(bn_neg_scale, ct),
                 )
 
-            def centre_and_gain(j, b):
-                i = j * B + b
-                o = xa[j][:, b, :]
-                squares = junk.tile([P, D], BF16)
-                nc.scalar.activation(
-                    out=squares[:], in_=o, func=ACT.Square, bias=neg_mean[:, i : i + 1], scale=1.0, accum_out=sum_sq[:, i : i + 1]
-                )
-                nc.scalar.activation(
-                    out=ln_rstd[:, i : i + 1], in_=sum_sq[:, i : i + 1], func=ACT.Abs_reciprocal_sqrt, bias=eps[:], scale=1.0 / D
-                )
-                res = rowp.tile([P, D], F32)
+        def normalise(ct, j):
+            pair = slabs.tile([P, 2, GROUP], F32, tag="slab", name="pair", align_bytes=64)
+            nc.scalar.activation(
+                out=pair[:, 0, :], in_=y_tiles[ct, j][:], func=ACT.Identity, bias=col(bn_shift, ct), scale=col(bn_scale, ct)
+            )
+            zn[ct, j] = pair
+
+        def negative_part(ct, j):
+            pair = zn[ct, j]
+            nc.vector.tensor_scalar(
+                out=pair[:, 1, :], in0=pair[:, 0, :], scalar1=0.0, scalar2=slope_less_1[:], op0=ALU.min, op1=ALU.mult
+            )
+
+        x_tiles = {}
+        a_tiles = {}
+        o_tiles = {}
+        res_v = {}
+        res_tiles = {}
+        ln_gain = {}
+
+        def load_streams(i):
+            j, b = divmod(i, B)
+            x_t = streams.tile([P, D], BF16)
+            nc.sync.dma_start(out=x_t[:], in_=x[j * P : (j + 1) * P, b, :])
+            a_t = streams.tile([P, D], BF16)
+            nc.sync.dma_start(out=a_t[:], in_=res_a[b, j * P : (j + 1) * P, :])
+            x_tiles[i], a_tiles[i] = x_t, a_t
+
+        def add_streams(i):
+            o = rows_pool.tile([P, D], F32, tag="o", name="o")
+            nc.gpsimd.tensor_tensor(out=o[:], in0=x_tiles[i][:], in1=a_tiles[i][:], op=ALU.add)
+            o_tiles[i] = o
+
+        def to_rows(i, half):
+            j, b = divmod(i, B)
+            rows = slice(b * P, (b + 1) * P)
+            res = bank("res")
+            if i >= GP_SUMS:
+                a_half = a_tiles[i][:, half * BANK : (half + 1) * BANK]
+                nc.tensor.matmul(res[:], lhsT=ident_bf[:], rhs=a_half, start=True, stop=False)
+            for q in range(TILES):
+                pair = zn[half * TILES + q, j]
+                cells = res[:, q * P : (q + 1) * P]
+                last = q == TILES - 1 if i >= GP_SUMS else True
+                nc.tensor.matmul(cells, lhsT=pair[:, 0, rows], rhs=ident[:], is_transpose=True, start=(i < GP_SUMS), stop=False)
+                nc.tensor.matmul(cells, lhsT=pair[:, 1, rows], rhs=ident[:], is_transpose=True, start=False, stop=last)
+            res_v[i, half] = res
+
+        def sum_of_streams(i, half):
+            cols = slice(half * BANK, (half + 1) * BANK)
+            if i < GP_SUMS:
+                other = o_tiles[i]
+            else:
+                other = x_tiles[i]
+                if half == 0:
+                    o = rows_pool.tile([P, D], F32, tag="o", name="o")
+                    o_tiles[i] = o
+            nc.vector.scalar_tensor_tensor(
+                out=o_tiles[i][:, cols], in0=res_v[i, half][:], scalar=1.0, in1=other[:, cols], op0=ALU.mult, op1=ALU.add,
+                accum_out=row_sum[:, i, half : half + 1],
+            )
+
+        def mean(i):
+            nc.vector.tensor_scalar(
+                out=col(neg_mean, i), in0=row_sum[:, i, 0:1], scalar1=row_sum[:, i, 1:2], scalar2=-1.0 / D,
+                op0=ALU.add, op1=ALU.mult,
+            )
+
+        def centre_and_gain(i, half):
+            cols = slice(half * BANK, (half + 1) * BANK)
+            if half == 0:
+                res = res_pool.tile([P, D], F32)
+                res_tiles[i] = res
+            nc.vector.scalar_tensor_tensor(
+                out=res_tiles[i][:, cols], in0=o_tiles[i][:, cols], scalar=col(neg_mean, i), in1=ln_gain[half][:],
+                op0=ALU.add, op1=ALU.mult,
+            )
+
+        def squares(i):
+            junk = junk_pool.tile([P, D], BF16)
+            nc.scalar.activation(
+                out=junk[:], in_=o_tiles[i][:], func=ACT.Square, bias=col(neg_mean, i), scale=1.0, accum_out=col(sum_sq, i)
+            )
+
+        def row_rstd(i):
+            nc.scalar.activation(
+                out=col(ln_rstd, i), in_=col(sum_sq, i), func=ACT.Abs_reciprocal_sqrt, bias=eps[:], scale=1.0 / D
+            )
+
+        def finish(i):
+            j, b = divmod(i, B)
+            res = res_tiles[i]
+            if i == ROW_TILES - 1:
                 for half in range(HALVES):
                     cols = slice(half * BANK, (half + 1) * BANK)
                     nc.vector.scalar_tensor_tensor(
-                        out=res[:, cols], in0=o[:, cols], scalar=neg_mean[:, i : i + 1], in1=ln_gain[half][:], op0=ALU.add, op1=ALU.mult
+                        out=res[:, cols], in0=res[:, cols], scalar=col(ln_rstd, i), in1=ln_bias[:, cols], op0=ALU.mult, op1=ALU.add
                     )
-                res_tiles[i] = res
-
-            def scale_bias_store(j, b):
-                i = j * B + b
-                res = res_tiles[i]
-                nc.scalar.activation(out=res[:], in_=res[:], func=ACT.Copy, scale=ln_rstd[:, i : i + 1])
+                    nc.sync.dma_start(out=out[j * P : (j + 1) * P, b, cols], in_=res[:, cols])
+            else:
+                nc.scalar.activation(out=res[:], in_=res[:], func=ACT.Copy, scale=col(ln_rstd, i))
                 nc.gpsimd.tensor_tensor(out=res[:], in0=res[:], in1=ln_bias[:], op=ALU.add)
                 nc.sync.dma_start(out=out[j * P : (j + 1) * P, b, :], in_=res[:])
 
-            for ct in range(0, C_TILES, 2):
-                batch_norm_prelu(0, ct)
-            for i in range(ROW_TILES):
-                j, b = divmod(i, B)
-                sum_of_streams(j, b)
-                if j + 1 < L_TILES:
-                    batch_norm_prelu(j + 1, 2 * b)
-                if i > 0:
-                    scale_bias_store(*divmod(i - 1, B))
-                centre_and_gain(j, b)
-            scale_bias_store(L_TILES - 1, B - 1)
+        prepare_group(0)
+        prepare_group(1)
+        nc.vector.tensor_scalar_add(out=slope_less_1[:], in0=slope[:], scalar1=-1.0)
+        bn_cols = psum.tile([P, P], BF16, tag="bank", name="bn_cols")
+        nc.tensor.transpose(bn_cols[:], bn_rows[:], ident_bf[:])
+        nc.vector.tensor_copy(out=bn_gain_bias[:], in_=bn_cols[:, 0 : 2 * C_TILES])
+        nc.vector.tensor_scalar_mul(out=neg_gain[:], in0=bn_gain_bias[:, 0:C_TILES], scalar1=-1.0)
+        prepare_group(2)
+        product(0, 0)
+        for half in range(HALVES):
+            bias_ps = bank("bias_ps")
+            first = D + half * BANK
+            nc.tensor.matmul(bias_ps[:], lhsT=ones_bf[:], rhs=ln_rows[:, first : first + BANK], start=True, stop=True)
+            nc.scalar.copy(out=ln_bias[:, half * BANK : (half + 1) * BANK], in_=bias_ps[:])
+        statistics(0, 0)
+        prepare_group(3)
+        for i in range(STREAMS):
+            load_streams(i)
+        product(0, 1)
+        statistics(0, 1)
+        prepare_group(4)
+        product(0, 2)
+        statistics(0, 2)
+        prepare_group(5)
+        product(0, 3)
+        statistics(0, 3)
+        for step in range(3):
+            bn_prepare(0, step)
+        for j in range(L_TILES):
+            product(1, j)
+            statistics(1, j)
+        summed = 0
+        for ct in range(C_TILES):
+            for j in range(L_TILES):
+                normalise(ct, j)
+                if ct + 2 < C_TILES:
+                    product(ct + 2, j)
+                elif ct + 2 == C_TILES:
+                    to_rows(j, 0)
+                if ct + 1 < C_TILES and j > 0:
+                    bn_prepare(ct + 1, j - 1)
+                if j < L_TILES - 1:
+                    negative_part(ct, j)
+                    if ct + 2 < C_TILES:
+                        statistics(ct + 2, j)
+            negative_part(ct, L_TILES - 1)
+            if ct + 2 < C_TILES:
+                statistics(ct + 2, L_TILES - 1)
+            elif ct + 2 == C_TILES:
+                for i in range(B):
+                    sum_of_streams(i, 0)
+            if ct > 0 and summed < GP_SUMS:
+                add_streams(summed)
+                if summed + STREAMS < ROW_TILES:
+                    load_streams(summed + STREAMS)
+                summed += 1
+
+        for i in range(ROW_TILES):
+            if i >= B:
+                to_rows(i, 0)
+            to_rows(i, 1)
+            if i == 0:
+                for half in range(HALVES):
+                    gain = bank("gain")
+                    nc.tensor.matmul(
+                        gain[:], lhsT=ones_bf[:], rhs=ln_rows[:, half * BANK : (half + 1) * BANK], start=True, stop=True
+                    )
+                    ln_gain[half] = gain
+            if i >= B:
+                sum_of_streams(i, 0)
+            if i > 0:
+                centre_and_gain(i - 1, 0)
+            sum_of_streams(i, 1)
+            if i > 0:
+                centre_and_gain(i - 1, 1)
+            mean(i)
+            if i >= GP_SUMS and i + STREAMS < ROW_TILES:
+                load_streams(i + STREAMS)
+            squares(i)
+            if i > 0:
+                finish(i - 1)
+            row_rstd(i)
+        for half in range(HALVES):
+            centre_and_gain(ROW_TILES - 1, half)
+        finish(ROW_TILES - 1)

@@ -36,24 +36,25 @@ def tile_coattention_pb_kernel(tc, x, res_a, ctx_v, W_v, bn_v_g, bn_v_b, prelu_v
     with ExitStack() as whole:
         whole.enter_context(tc.manual_schedule())
         const = whole.enter_context(tc.tile_pool(name="const", bufs=1))
-        slabs = whole.enter_context(tc.tile_pool(name="slabs", bufs=L_TILES * C_TILES + 1))
+        slabs = whole.enter_context(tc.tile_pool(name="slabs", bufs=2 * C_TILES + 1))
         streams = whole.enter_context(tc.tile_pool(name="streams", bufs=STREAMS))
         rows_pool = whole.enter_context(tc.tile_pool(name="rows_pool", bufs=O_BUFS))
         res_pool = whole.enter_context(tc.tile_pool(name="res_pool", bufs=4))
-        junk_pool = whole.enter_context(tc.tile_pool(name="junk_pool", bufs=2))
+        junk_pool = whole.enter_context(tc.tile_pool(name="junk_pool", bufs=1))
         mx = whole.enter_context(tc.tile_pool(name="mx", bufs=1))
         psum = whole.enter_context(tc.psum_pool(name="psum", bufs=8))
 
         w_rows = [W_v[h * GROUP : (h + 1) * GROUP, :].rearrange("(r p) k -> p r k", p=P) for h in range(W_GROUPS)]
         c_rows = [ctx_v[:, j * P : (j + 1) * P, :].rearrange("b l k -> l b k") for j in range(L_TILES)]
-        sources = [w_rows[0]] + c_rows + [w_rows[1]]
+        sources = w_rows + c_rows
         raw_tiles = {}
 
         def load_group(s):
+            raw = slabs.tile([P, TILES, D], BF16, tag="slab", name="raw", align_bytes=64)
             for hf in range(2):
-                raw = slabs.tile([P, 2, D], BF16, tag="slab", name="raw", align_bytes=64)
-                nc.sync.dma_start(out=raw[:], in_=sources[s][:, 2 * hf : 2 * hf + 2, :])
-                raw_tiles[s, hf] = raw
+                r = slice(2 * hf, 2 * hf + 2)
+                nc.sync.dma_start(out=raw[:, r, :], in_=sources[s][:, r, :])
+            raw_tiles[s] = raw
 
         for s in range(DEPTH):
             load_group(s)
@@ -104,16 +105,14 @@ def tile_coattention_pb_kernel(tc, x, res_a, ctx_v, W_v, bn_v_g, bn_v_b, prelu_v
         def prepare_group(s):
             codes = mx.tile([P, PASSES, GROUP], U32, name="codes%d" % s, align_bytes=64)
             scales = mx.tile([P, PASSES, GROUP], U8, name="scales%d" % s, align_bytes=64)
-            staged = []
+            grouped = slabs.tile([P, PASSES, GROUP * 4], BF16, tag="slab", name="grouped", align_bytes=64)
             for g in range(PASSES):
-                grouped = slabs.tile([P, GROUP * 4], BF16, tag="slab", name="grouped", align_bytes=64)
-                staged.append(grouped)
-                words_out = grouped[:].bitcast(F32).rearrange("p (q r u) -> p q r u", q=2, u=2)
+                words_out = grouped[:, g, :].bitcast(F32).rearrange("p (q r u) -> p q r u", q=2, u=2)
                 for hf in range(2):
                     xt = bank("xt")
                     planes = xt[:].rearrange("p (t u r) -> p t u r", t=2, u=2)
                     for t in range(2):
-                        words = raw_tiles[s, hf][:, t, :].bitcast(F32)
+                        words = raw_tiles[s][:, 2 * hf + t, :].bitcast(F32)
                         for u in range(2):
                             first = (2 * g + u) * P
                             nc.tensor.transpose(planes[:, t, u, :], words[:, first : first + P], ident[:])
@@ -126,7 +125,7 @@ def tile_coattention_pb_kernel(tc, x, res_a, ctx_v, W_v, bn_v_g, bn_v_b, prelu_v
             if s + DEPTH < len(sources):
                 load_group(s + DEPTH)
             for g in range(PASSES):
-                nc.vector.quantize_mx(out=codes[:, g, :].bitcast(FP8X4), scales=scales[:, g, :], in_=staged[g][:])
+                nc.vector.quantize_mx(out=codes[:, g, :].bitcast(FP8X4), scales=scales[:, g, :], in_=grouped[:, g, :])
             mx_tiles[s] = (codes, scales)
 
         y_tiles = {}
@@ -134,8 +133,8 @@ def tile_coattention_pb_kernel(tc, x, res_a, ctx_v, W_v, bn_v_g, bn_v_b, prelu_v
 
         def product(ct, j):
             h, q = divmod(ct, TILES)
-            w_codes, w_scales = mx_tiles[0 if h == 0 else L_TILES + 1]
-            c_codes, c_scales = mx_tiles[1 + j]
+            w_codes, w_scales = mx_tiles[h]
+            c_codes, c_scales = mx_tiles[W_GROUPS + j]
             cols = slice(q * P, (q + 1) * P)
             y = bank("y")
             for g in range(PASSES):
@@ -173,16 +172,18 @@ def tile_coattention_pb_kernel(tc, x, res_a, ctx_v, W_v, bn_v_g, bn_v_b, prelu_v
                 )
 
         def normalise(ct, j):
-            pair = slabs.tile([P, 2, GROUP], F32, tag="slab", name="pair", align_bytes=64)
+            if j % 2 == 0:
+                two = slabs.tile([P, 2, 2, GROUP], F32, tag="slab", name="two", align_bytes=64)
+                zn[ct, j // 2] = two
             nc.scalar.activation(
-                out=pair[:, 0, :], in_=y_tiles[ct, j][:], func=ACT.Identity, bias=col(bn_shift, ct), scale=col(bn_scale, ct)
+                out=zn[ct, j // 2][:, 0, j % 2, :], in_=y_tiles[ct, j][:], func=ACT.Identity,
+                bias=col(bn_shift, ct), scale=col(bn_scale, ct),
             )
-            zn[ct, j] = pair
 
-        def negative_part(ct, j):
-            pair = zn[ct, j]
+        def negative_part(ct, jj):
+            two = zn[ct, jj]
             nc.vector.tensor_scalar(
-                out=pair[:, 1, :], in0=pair[:, 0, :], scalar1=0.0, scalar2=slope_less_1[:], op0=ALU.min, op1=ALU.mult
+                out=two[:, 1, :, :], in0=two[:, 0, :, :], scalar1=0.0, scalar2=slope_less_1[:], op0=ALU.min, op1=ALU.mult
             )
 
         x_tiles = {}
@@ -202,7 +203,9 @@ def tile_coattention_pb_kernel(tc, x, res_a, ctx_v, W_v, bn_v_g, bn_v_b, prelu_v
 
         def add_streams(i):
             o = rows_pool.tile([P, D], F32, tag="o", name="o")
-            nc.gpsimd.tensor_tensor(out=o[:], in0=x_tiles[i][:], in1=a_tiles[i][:], op=ALU.add)
+            for half in range(HALVES):
+                cols = slice(half * BANK, (half + 1) * BANK)
+                nc.gpsimd.tensor_tensor(out=o[:, cols], in0=x_tiles[i][:, cols], in1=a_tiles[i][:, cols], op=ALU.add)
             o_tiles[i] = o
 
         def to_rows(i, half):
@@ -213,11 +216,11 @@ def tile_coattention_pb_kernel(tc, x, res_a, ctx_v, W_v, bn_v_g, bn_v_b, prelu_v
                 a_half = a_tiles[i][:, half * BANK : (half + 1) * BANK]
                 nc.tensor.matmul(res[:], lhsT=ident_bf[:], rhs=a_half, start=True, stop=False)
             for q in range(TILES):
-                pair = zn[half * TILES + q, j]
+                two = zn[half * TILES + q, j // 2]
                 cells = res[:, q * P : (q + 1) * P]
                 last = q == TILES - 1 if i >= GP_SUMS else True
-                nc.tensor.matmul(cells, lhsT=pair[:, 0, rows], rhs=ident[:], is_transpose=True, start=(i < GP_SUMS), stop=False)
-                nc.tensor.matmul(cells, lhsT=pair[:, 1, rows], rhs=ident[:], is_transpose=True, start=False, stop=last)
+                nc.tensor.matmul(cells, lhsT=two[:, 0, j % 2, rows], rhs=ident[:], is_transpose=True, start=(i < GP_SUMS), stop=False)
+                nc.tensor.matmul(cells, lhsT=two[:, 1, j % 2, rows], rhs=ident[:], is_transpose=True, start=False, stop=last)
             res_v[i, half] = res
 
         def sum_of_streams(i, half):
@@ -284,24 +287,19 @@ def tile_coattention_pb_kernel(tc, x, res_a, ctx_v, W_v, bn_v_g, bn_v_b, prelu_v
         nc.vector.tensor_copy(out=bn_gain_bias[:], in_=bn_cols[:, 0 : 2 * C_TILES])
         nc.vector.tensor_scalar_mul(out=neg_gain[:], in0=bn_gain_bias[:, 0:C_TILES], scalar1=-1.0)
         prepare_group(2)
-        product(0, 0)
         for half in range(HALVES):
             bias_ps = bank("bias_ps")
             first = D + half * BANK
             nc.tensor.matmul(bias_ps[:], lhsT=ones_bf[:], rhs=ln_rows[:, first : first + BANK], start=True, stop=True)
             nc.scalar.copy(out=ln_bias[:, half * BANK : (half + 1) * BANK], in_=bias_ps[:])
-        statistics(0, 0)
-        prepare_group(3)
+        for j in range(1, L_TILES):
+            prepare_group(W_GROUPS + j)
+            product(0, j - 1)
+            statistics(0, j - 1)
         for i in range(STREAMS):
             load_streams(i)
-        product(0, 1)
-        statistics(0, 1)
-        prepare_group(4)
-        product(0, 2)
-        statistics(0, 2)
-        prepare_group(5)
-        product(0, 3)
-        statistics(0, 3)
+        product(0, L_TILES - 1)
+        statistics(0, L_TILES - 1)
         for step in range(3):
             bn_prepare(0, step)
         for j in range(L_TILES):
@@ -317,16 +315,14 @@ def tile_coattention_pb_kernel(tc, x, res_a, ctx_v, W_v, bn_v_g, bn_v_b, prelu_v
                     to_rows(j, 0)
                 if ct + 1 < C_TILES and j > 0:
                     bn_prepare(ct + 1, j - 1)
-                if j < L_TILES - 1:
-                    negative_part(ct, j)
+                if j % 2 == 1:
+                    negative_part(ct, j // 2)
                     if ct + 2 < C_TILES:
+                        statistics(ct + 2, j - 1)
                         statistics(ct + 2, j)
-            negative_part(ct, L_TILES - 1)
-            if ct + 2 < C_TILES:
-                statistics(ct + 2, L_TILES - 1)
-            elif ct + 2 == C_TILES:
-                for i in range(B):
-                    sum_of_streams(i, 0)
+                    elif ct + 2 == C_TILES:
+                        sum_of_streams(j - 1, 0)
+                        sum_of_streams(j, 0)
             if ct > 0 and summed < GP_SUMS:
                 add_streams(summed)
                 if summed + STREAMS < ROW_TILES:

@@ -82,16 +82,18 @@ def tile_coattention_pb_kernel(tc, x, res_a, ctx_v, W_v, bn_v_g, bn_v_b, prelu_v
         nc.scalar.dma_start(out=ln_rows[0:1, D : 2 * D], in_=ln_b.rearrange("(o c) -> o c", o=1))
 
         slope_less_1 = const.tile([P, 1], F32)
+        sign = const.tile([P, 1], F32)
+        ident_sign = const.tile([P, P], BF16)
         bn_gain_bias = const.tile([P, 2 * C_TILES], F32)
         neg_gain = const.tile([P, C_TILES], F32)
         ln_bias = const.tile([P, D], F32)
         stats = const.tile([P, C_TILES, L_TILES, 6], F32)
         mean_var = const.tile([P, C_TILES, 2], F32)
         bn_rstd = const.tile([P, C_TILES], F32)
-        bn_scale = const.tile([P, C_TILES], F32)
-        bn_neg_scale = const.tile([P, C_TILES], F32)
-        bn_shift = const.tile([P, C_TILES], F32)
+        neg_mean_gain = const.tile([P, C_TILES], F32)
+        affine = const.tile([P, C_TILES, 2], F32)
         row_sum = const.tile([P, ROW_TILES, HALVES], F32)
+        scaled_sums = const.tile([P, ROW_TILES, HALVES], F32)
         neg_mean = const.tile([P, ROW_TILES], F32)
         sum_sq = const.tile([P, ROW_TILES], F32)
         ln_rstd = const.tile([P, ROW_TILES], F32)
@@ -118,7 +120,7 @@ def tile_coattention_pb_kernel(tc, x, res_a, ctx_v, W_v, bn_v_g, bn_v_b, prelu_v
                             nc.tensor.transpose(planes[:, t, u, :], words[:, first : first + P], ident[:])
                     src = planes.rearrange("p t u r -> p t r u")
                     dst = words_out[:, hf, :, :].rearrange("p (t r) u -> p t r u", t=2)
-                    if g == PASSES - 1 and hf == 1:
+                    if g == PASSES - 1 and hf == 0:
                         nc.vector.tensor_copy(out=dst, in_=src)
                     else:
                         nc.scalar.copy(out=dst, in_=src)
@@ -162,13 +164,13 @@ def tile_coattention_pb_kernel(tc, x, res_a, ctx_v, W_v, bn_v_g, bn_v_b, prelu_v
                 nc.scalar.activation(
                     out=col(bn_rstd, ct), in_=mean_var[:, ct, 1:2], func=ACT.Abs_reciprocal_sqrt, bias=eps[:], scale=1.0
                 )
-            elif step == 1:
-                nc.scalar.activation(out=col(bn_neg_scale, ct), in_=col(bn_rstd, ct), func=ACT.Copy, scale=col(neg_gain, ct))
-                nc.scalar.activation(out=col(bn_scale, ct), in_=col(bn_rstd, ct), func=ACT.Copy, scale=col(bn_gain_bias, ct))
+                nc.scalar.activation(out=col(neg_mean_gain, ct), in_=mean_var[:, ct, 0:1], func=ACT.Copy, scale=col(neg_gain, ct))
             else:
+                rstd = col(bn_rstd, ct)
+                nc.scalar.activation(out=affine[:, ct, 0:1], in_=col(bn_gain_bias, ct), func=ACT.Copy, scale=rstd)
                 nc.scalar.activation(
-                    out=col(bn_shift, ct), in_=mean_var[:, ct, 0:1], func=ACT.Identity,
-                    bias=col(bn_gain_bias, C_TILES + ct), scale=col(bn_neg_scale, ct),
+                    out=affine[:, ct, 1:2], in_=col(neg_mean_gain, ct), func=ACT.Identity,
+                    bias=col(bn_gain_bias, C_TILES + ct), scale=rstd,
                 )
 
         def normalise(ct, j):
@@ -177,14 +179,17 @@ def tile_coattention_pb_kernel(tc, x, res_a, ctx_v, W_v, bn_v_g, bn_v_b, prelu_v
                 zn[ct, j // 2] = two
             nc.scalar.activation(
                 out=zn[ct, j // 2][:, 0, j % 2, :], in_=y_tiles[ct, j][:], func=ACT.Identity,
-                bias=col(bn_shift, ct), scale=col(bn_scale, ct),
+                bias=affine[:, ct, 1:2], scale=affine[:, ct, 0:1],
             )
 
-        def negative_part(ct, jj):
+        def second_term(ct, jj):
             two = zn[ct, jj]
-            nc.vector.tensor_scalar(
-                out=two[:, 1, :, :], in0=two[:, 0, :, :], scalar1=0.0, scalar2=slope_less_1[:], op0=ALU.min, op1=ALU.mult
-            )
+            if ct % 2 == 1 and jj == 1:
+                nc.scalar.activation(out=two[:, 1, :, :], in_=two[:, 0, :, :], func=ACT.Relu, scale=slope_less_1[:])
+            else:
+                nc.vector.tensor_scalar(
+                    out=two[:, 1, :, :], in0=two[:, 0, :, :], scalar1=slope_less_1[:], scalar2=0.0, op0=ALU.mult, op1=ALU.max
+                )
 
         x_tiles = {}
         a_tiles = {}
@@ -214,7 +219,7 @@ def tile_coattention_pb_kernel(tc, x, res_a, ctx_v, W_v, bn_v_g, bn_v_b, prelu_v
             res = bank("res")
             if i >= GP_SUMS:
                 a_half = a_tiles[i][:, half * BANK : (half + 1) * BANK]
-                nc.tensor.matmul(res[:], lhsT=ident_bf[:], rhs=a_half, start=True, stop=False)
+                nc.tensor.matmul(res[:], lhsT=ident_sign[:], rhs=a_half, start=True, stop=False)
             for q in range(TILES):
                 two = zn[half * TILES + q, j // 2]
                 cells = res[:, q * P : (q + 1) * P]
@@ -233,14 +238,13 @@ def tile_coattention_pb_kernel(tc, x, res_a, ctx_v, W_v, bn_v_g, bn_v_b, prelu_v
                     o = rows_pool.tile([P, D], F32, tag="o", name="o")
                     o_tiles[i] = o
             nc.vector.scalar_tensor_tensor(
-                out=o_tiles[i][:, cols], in0=res_v[i, half][:], scalar=1.0, in1=other[:, cols], op0=ALU.mult, op1=ALU.add,
+                out=o_tiles[i][:, cols], in0=res_v[i, half][:], scalar=sign[:], in1=other[:, cols], op0=ALU.mult, op1=ALU.add,
                 accum_out=row_sum[:, i, half : half + 1],
             )
 
         def mean(i):
-            nc.vector.tensor_scalar(
-                out=col(neg_mean, i), in0=row_sum[:, i, 0:1], scalar1=row_sum[:, i, 1:2], scalar2=-1.0 / D,
-                op0=ALU.add, op1=ALU.mult,
+            nc.scalar.activation(
+                out=scaled_sums[:, i, :], in_=row_sum[:, i, :], func=ACT.Copy, scale=-1.0 / D, accum_out=col(neg_mean, i)
             )
 
         def centre_and_gain(i, half):
@@ -264,27 +268,35 @@ def tile_coattention_pb_kernel(tc, x, res_a, ctx_v, W_v, bn_v_g, bn_v_b, prelu_v
                 out=col(ln_rstd, i), in_=col(sum_sq, i), func=ACT.Abs_reciprocal_sqrt, bias=eps[:], scale=1.0 / D
             )
 
-        def finish(i):
+        def scale_rows(i, half):
+            cols = slice(half * BANK, (half + 1) * BANK)
+            nc.scalar.activation(out=res_tiles[i][:, cols], in_=res_tiles[i][:, cols], func=ACT.Copy, scale=col(ln_rstd, i))
+
+        def bias_store(i):
             j, b = divmod(i, B)
             res = res_tiles[i]
-            if i == ROW_TILES - 1:
-                for half in range(HALVES):
-                    cols = slice(half * BANK, (half + 1) * BANK)
-                    nc.vector.scalar_tensor_tensor(
-                        out=res[:, cols], in0=res[:, cols], scalar=col(ln_rstd, i), in1=ln_bias[:, cols], op0=ALU.mult, op1=ALU.add
-                    )
-                    nc.sync.dma_start(out=out[j * P : (j + 1) * P, b, cols], in_=res[:, cols])
-            else:
-                nc.scalar.activation(out=res[:], in_=res[:], func=ACT.Copy, scale=col(ln_rstd, i))
-                nc.gpsimd.tensor_tensor(out=res[:], in0=res[:], in1=ln_bias[:], op=ALU.add)
-                nc.sync.dma_start(out=out[j * P : (j + 1) * P, b, :], in_=res[:])
+            nc.gpsimd.tensor_tensor(out=res[:], in0=res[:], in1=ln_bias[:], op=ALU.add)
+            nc.sync.dma_start(out=out[j * P : (j + 1) * P, b, :], in_=res[:])
+
+        def scale_bias_store(i):
+            j, b = divmod(i, B)
+            res = res_tiles[i]
+            for half in range(HALVES):
+                cols = slice(half * BANK, (half + 1) * BANK)
+                nc.vector.scalar_tensor_tensor(
+                    out=res[:, cols], in0=res[:, cols], scalar=col(ln_rstd, i), in1=ln_bias[:, cols], op0=ALU.mult, op1=ALU.add
+                )
+                nc.sync.dma_start(out=out[j * P : (j + 1) * P, b, cols], in_=res[:, cols])
 
         prepare_group(0)
         prepare_group(1)
         nc.vector.tensor_scalar_add(out=slope_less_1[:], in0=slope[:], scalar1=-1.0)
+        nc.vector.tensor_scalar(out=sign[:], in0=slope_less_1[:], scalar1=0.0, scalar2=2.0, op0=ALU.is_le, op1=ALU.mult)
+        nc.vector.tensor_scalar_add(out=sign[:], in0=sign[:], scalar1=-1.0)
+        nc.vector.tensor_scalar_mul(out=ident_sign[:], in0=ident_bf[:], scalar1=sign[:])
         bn_cols = psum.tile([P, P], BF16, tag="bank", name="bn_cols")
         nc.tensor.transpose(bn_cols[:], bn_rows[:], ident_bf[:])
-        nc.vector.tensor_copy(out=bn_gain_bias[:], in_=bn_cols[:, 0 : 2 * C_TILES])
+        nc.vector.tensor_scalar_mul(out=bn_gain_bias[:], in0=bn_cols[:, 0 : 2 * C_TILES], scalar1=sign[:])
         nc.vector.tensor_scalar_mul(out=neg_gain[:], in0=bn_gain_bias[:, 0:C_TILES], scalar1=-1.0)
         prepare_group(2)
         for half in range(HALVES):
@@ -300,7 +312,7 @@ def tile_coattention_pb_kernel(tc, x, res_a, ctx_v, W_v, bn_v_g, bn_v_b, prelu_v
             load_streams(i)
         product(0, L_TILES - 1)
         statistics(0, L_TILES - 1)
-        for step in range(3):
+        for step in range(2):
             bn_prepare(0, step)
         for j in range(L_TILES):
             product(1, j)
@@ -313,16 +325,14 @@ def tile_coattention_pb_kernel(tc, x, res_a, ctx_v, W_v, bn_v_g, bn_v_b, prelu_v
                     product(ct + 2, j)
                 elif ct + 2 == C_TILES:
                     to_rows(j, 0)
-                if ct + 1 < C_TILES and j > 0:
-                    bn_prepare(ct + 1, j - 1)
-                if j % 2 == 1:
-                    negative_part(ct, j // 2)
-                    if ct + 2 < C_TILES:
-                        statistics(ct + 2, j - 1)
-                        statistics(ct + 2, j)
-                    elif ct + 2 == C_TILES:
-                        sum_of_streams(j - 1, 0)
-                        sum_of_streams(j, 0)
+                if ct + 1 < C_TILES and j > 1:
+                    bn_prepare(ct + 1, j - 2)
+                if ct + 2 < C_TILES:
+                    statistics(ct + 2, j)
+                elif ct + 2 == C_TILES:
+                    sum_of_streams(j, 0)
+            for jj in range(L_TILES // 2):
+                second_term(ct, jj)
             if ct > 0 and summed < GP_SUMS:
                 add_streams(summed)
                 if summed + STREAMS < ROW_TILES:
@@ -350,10 +360,13 @@ def tile_coattention_pb_kernel(tc, x, res_a, ctx_v, W_v, bn_v_g, bn_v_b, prelu_v
             mean(i)
             if i >= GP_SUMS and i + STREAMS < ROW_TILES:
                 load_streams(i + STREAMS)
+            if i > 0:
+                scale_rows(i - 1, 0)
             squares(i)
             if i > 0:
-                finish(i - 1)
+                scale_rows(i - 1, 1)
+                bias_store(i - 1)
             row_rstd(i)
         for half in range(HALVES):
             centre_and_gain(ROW_TILES - 1, half)
-        finish(ROW_TILES - 1)
+        scale_bias_store(ROW_TILES - 1)

@@ -25,7 +25,7 @@ HALVES = D // BANK
 EPS = 1e-5
 DEPTH = 3
 STREAMS = 5
-GP_SUMS = 6
+GP_SUMS = 4
 O_BUFS = 6
 
 FLOPS = 2 * L * B * D * D
@@ -63,28 +63,23 @@ def tile_coattention_pb_kernel(tc, x, res_a, ctx_v, W_v, bn_v_g, bn_v_b, prelu_v
         make_identity(nc, ident[:])
         ident_bf = const.tile([P, P], BF16)
         make_identity(nc, ident_bf[:])
-        ones_bf = const.tile([P, P], BF16)
-        nc.vector.memset(ones_bf[:], 1.0)
         eps = const.tile([P, 1], F32)
         nc.vector.memset(eps[:], EPS)
         table_first = const.tile([P, 1], F32)
         nc.scalar.activation(out=table_first[:], in_=eps[:], func=ACT.Abs_reciprocal_sqrt)
 
-        bn_rows = const.tile([P, P], BF16)
-        nc.vector.memset(bn_rows[:], 0.0)
-        ln_rows = const.tile([P, 2 * D], BF16)
-        nc.vector.memset(ln_rows[:], 0.0)
+        vector_rows = const.tile([P, P], BF16)
+        nc.vector.memset(vector_rows[:], 0.0)
         slope = const.tile([P, 1], BF16)
         nc.scalar.dma_start(out=slope[:], in_=prelu_v.partition_broadcast(P))
-        nc.scalar.dma_start(out=bn_rows[0:C_TILES, :], in_=bn_v_g.rearrange("(t c) -> t c", t=C_TILES))
-        nc.scalar.dma_start(out=bn_rows[C_TILES : 2 * C_TILES, :], in_=bn_v_b.rearrange("(t c) -> t c", t=C_TILES))
-        nc.scalar.dma_start(out=ln_rows[0:1, 0:D], in_=ln_g.rearrange("(o c) -> o c", o=1))
-        nc.scalar.dma_start(out=ln_rows[0:1, D : 2 * D], in_=ln_b.rearrange("(o c) -> o c", o=1))
+        for v, vector in enumerate((bn_v_g, bn_v_b, ln_g, ln_b)):
+            nc.scalar.dma_start(out=vector_rows[v * C_TILES : (v + 1) * C_TILES, :], in_=vector.rearrange("(t c) -> t c", t=C_TILES))
 
         slope_less_1 = const.tile([P, 1], F32)
         sign = const.tile([P, 1], F32)
         ident_sign = const.tile([P, P], BF16)
         bn_gain_bias = const.tile([P, 2 * C_TILES], F32)
+        ln_gain_bias = const.tile([P, 2 * C_TILES], F32)
         neg_gain = const.tile([P, C_TILES], F32)
         ln_bias = const.tile([P, D], F32)
         stats = const.tile([P, C_TILES, L_TILES, 6], F32)
@@ -97,6 +92,13 @@ def tile_coattention_pb_kernel(tc, x, res_a, ctx_v, W_v, bn_v_g, bn_v_b, prelu_v
         neg_mean = const.tile([P, ROW_TILES], F32)
         sum_sq = const.tile([P, ROW_TILES], F32)
         ln_rstd = const.tile([P, ROW_TILES], F32)
+
+        def spread(name, first):
+            tile = bank(name)
+            for q in range(TILES):
+                column = ln_gain_bias[:, first + q : first + q + 1].to_broadcast([P, P])
+                nc.tensor.transpose(tile[:, q * P : (q + 1) * P], column, ident[:])
+            return tile
 
         def bank(name):
             tile = psum.tile([P, BANK], F32, tag="bank", name=name)
@@ -289,21 +291,20 @@ def tile_coattention_pb_kernel(tc, x, res_a, ctx_v, W_v, bn_v_g, bn_v_b, prelu_v
                 nc.sync.dma_start(out=out[j * P : (j + 1) * P, b, cols], in_=res[:, cols])
 
         prepare_group(0)
-        prepare_group(1)
         nc.vector.tensor_scalar_add(out=slope_less_1[:], in0=slope[:], scalar1=-1.0)
         nc.vector.tensor_scalar(out=sign[:], in0=slope_less_1[:], scalar1=0.0, scalar2=2.0, op0=ALU.is_le, op1=ALU.mult)
+        vector_cols = psum.tile([P, P], BF16, tag="bank", name="vector_cols")
+        nc.tensor.transpose(vector_cols[:], vector_rows[:], ident_bf[:])
+        nc.vector.tensor_copy(out=ln_gain_bias[:], in_=vector_cols[:, 2 * C_TILES : 4 * C_TILES])
         nc.vector.tensor_scalar_add(out=sign[:], in0=sign[:], scalar1=-1.0)
+        prepare_group(1)
+        nc.vector.tensor_scalar_mul(out=bn_gain_bias[:], in0=vector_cols[:, 0 : 2 * C_TILES], scalar1=sign[:])
         nc.vector.tensor_scalar_mul(out=ident_sign[:], in0=ident_bf[:], scalar1=sign[:])
-        bn_cols = psum.tile([P, P], BF16, tag="bank", name="bn_cols")
-        nc.tensor.transpose(bn_cols[:], bn_rows[:], ident_bf[:])
-        nc.vector.tensor_scalar_mul(out=bn_gain_bias[:], in0=bn_cols[:, 0 : 2 * C_TILES], scalar1=sign[:])
         nc.vector.tensor_scalar_mul(out=neg_gain[:], in0=bn_gain_bias[:, 0:C_TILES], scalar1=-1.0)
-        prepare_group(2)
         for half in range(HALVES):
-            bias_ps = bank("bias_ps")
-            first = D + half * BANK
-            nc.tensor.matmul(bias_ps[:], lhsT=ones_bf[:], rhs=ln_rows[:, first : first + BANK], start=True, stop=True)
+            bias_ps = spread("bias_ps", C_TILES + half * TILES)
             nc.scalar.copy(out=ln_bias[:, half * BANK : (half + 1) * BANK], in_=bias_ps[:])
+        prepare_group(2)
         for j in range(1, L_TILES):
             prepare_group(W_GROUPS + j)
             product(0, j - 1)
@@ -345,11 +346,7 @@ def tile_coattention_pb_kernel(tc, x, res_a, ctx_v, W_v, bn_v_g, bn_v_b, prelu_v
             to_rows(i, 1)
             if i == 0:
                 for half in range(HALVES):
-                    gain = bank("gain")
-                    nc.tensor.matmul(
-                        gain[:], lhsT=ones_bf[:], rhs=ln_rows[:, half * BANK : (half + 1) * BANK], start=True, stop=True
-                    )
-                    ln_gain[half] = gain
+                    ln_gain[half] = spread("gain", half * TILES)
             if i >= B:
                 sum_of_streams(i, 0)
             if i > 0:

@@ -27,6 +27,7 @@ DEPTH = 3
 STREAMS = 5
 GP_SUMS = 4
 O_BUFS = 6
+LAG = 2
 
 FLOPS = 2 * L * B * D * D
 
@@ -39,7 +40,7 @@ def tile_coattention_pb_kernel(tc, x, res_a, ctx_v, W_v, bn_v_g, bn_v_b, prelu_v
         slabs = whole.enter_context(tc.tile_pool(name="slabs", bufs=2 * C_TILES + 1))
         streams = whole.enter_context(tc.tile_pool(name="streams", bufs=STREAMS))
         rows_pool = whole.enter_context(tc.tile_pool(name="rows_pool", bufs=O_BUFS))
-        res_pool = whole.enter_context(tc.tile_pool(name="res_pool", bufs=4))
+        res_pool = whole.enter_context(tc.tile_pool(name="res_pool", bufs=5))
         junk_pool = whole.enter_context(tc.tile_pool(name="junk_pool", bufs=1))
         mx = whole.enter_context(tc.tile_pool(name="mx", bufs=1))
         psum = whole.enter_context(tc.psum_pool(name="psum", bufs=8))
@@ -186,7 +187,7 @@ def tile_coattention_pb_kernel(tc, x, res_a, ctx_v, W_v, bn_v_g, bn_v_b, prelu_v
 
         def second_term(ct, jj):
             two = zn[ct, jj]
-            if ct % 2 == 1 and jj == 1:
+            if (ct, jj) in ((1, 1), (3, 1), (5, 1), (7, 1),):
                 nc.scalar.activation(out=two[:, 1, :, :], in_=two[:, 0, :, :], func=ACT.Relu, scale=slope_less_1[:])
             else:
                 nc.vector.tensor_scalar(
@@ -245,8 +246,9 @@ def tile_coattention_pb_kernel(tc, x, res_a, ctx_v, W_v, bn_v_g, bn_v_b, prelu_v
             )
 
         def mean(i):
-            nc.scalar.activation(
-                out=scaled_sums[:, i, :], in_=row_sum[:, i, :], func=ACT.Copy, scale=-1.0 / D, accum_out=col(neg_mean, i)
+            nc.vector.tensor_scalar(
+                out=scaled_sums[:, i, :], in0=row_sum[:, i, :], scalar1=-1.0 / D, scalar2=None, op0=ALU.mult, op1=ALU.add,
+                accum_out=col(neg_mean, i),
             )
 
         def centre_and_gain(i, half):
@@ -270,15 +272,15 @@ def tile_coattention_pb_kernel(tc, x, res_a, ctx_v, W_v, bn_v_g, bn_v_b, prelu_v
                 out=col(ln_rstd, i), in_=col(sum_sq, i), func=ACT.Abs_reciprocal_sqrt, bias=eps[:], scale=1.0 / D
             )
 
-        def scale_rows(i, half):
-            cols = slice(half * BANK, (half + 1) * BANK)
-            nc.scalar.activation(out=res_tiles[i][:, cols], in_=res_tiles[i][:, cols], func=ACT.Copy, scale=col(ln_rstd, i))
-
-        def bias_store(i):
+        def finish(i):
             j, b = divmod(i, B)
             res = res_tiles[i]
-            nc.gpsimd.tensor_tensor(out=res[:], in0=res[:], in1=ln_bias[:], op=ALU.add)
-            nc.sync.dma_start(out=out[j * P : (j + 1) * P, b, :], in_=res[:])
+            pieces = HALVES if i in (0, ROW_TILES - 2) else 1
+            for piece in range(pieces):
+                cols = slice(piece * (D // pieces), (piece + 1) * (D // pieces))
+                nc.scalar.activation(out=res[:, cols], in_=res[:, cols], func=ACT.Copy, scale=col(ln_rstd, i))
+                nc.gpsimd.tensor_tensor(out=res[:, cols], in0=res[:, cols], in1=ln_bias[:, cols], op=ALU.add)
+                nc.sync.dma_start(out=out[j * P : (j + 1) * P, b, cols], in_=res[:, cols])
 
         def scale_bias_store(i):
             j, b = divmod(i, B)
@@ -318,8 +320,18 @@ def tile_coattention_pb_kernel(tc, x, res_a, ctx_v, W_v, bn_v_g, bn_v_b, prelu_v
         for j in range(L_TILES):
             product(1, j)
             statistics(1, j)
-        summed = 0
+        quantised_word = const.tile([P, 1], U32)
+        nc.gpsimd.tensor_copy(out=quantised_word[:], in_=mx_tiles[len(sources) - 1][0][:, PASSES - 1, GROUP - 1 : GROUP])
+        for i in range(GP_SUMS):
+            add_streams(i)
+            load_streams(i + STREAMS)
+        PRE = {6:[[5,0]],7:[[6,0]]}
+        MID = {7:[[7,0]]}
+        POST = {2:[[0,0]],3:[[1,0],[0,1]],4:[[2,0],[3,0],[1,1]],5:[[4,0],[3,1]],6:[[2,1]],7:[[4,1],[5,1]]}
+        TAIL = [[6,1],[7,1]]
         for ct in range(C_TILES):
+            for c, jj in PRE.get(ct, ()):
+                second_term(c, jj)
             for j in range(L_TILES):
                 normalise(ct, j)
                 if ct + 2 < C_TILES:
@@ -332,13 +344,13 @@ def tile_coattention_pb_kernel(tc, x, res_a, ctx_v, W_v, bn_v_g, bn_v_b, prelu_v
                     statistics(ct + 2, j)
                 elif ct + 2 == C_TILES:
                     sum_of_streams(j, 0)
-            for jj in range(L_TILES // 2):
-                second_term(ct, jj)
-            if ct > 0 and summed < GP_SUMS:
-                add_streams(summed)
-                if summed + STREAMS < ROW_TILES:
-                    load_streams(summed + STREAMS)
-                summed += 1
+                if j == 1:
+                    for c, jj in MID.get(ct, ()):
+                        second_term(c, jj)
+            for c, jj in POST.get(ct, ()):
+                second_term(c, jj)
+        for c, jj in TAIL:
+            second_term(c, jj)
 
         for i in range(ROW_TILES):
             if i >= B:
@@ -349,20 +361,19 @@ def tile_coattention_pb_kernel(tc, x, res_a, ctx_v, W_v, bn_v_g, bn_v_b, prelu_v
                     ln_gain[half] = spread("gain", half * TILES)
             if i >= B:
                 sum_of_streams(i, 0)
-            if i > 0:
-                centre_and_gain(i - 1, 0)
             sum_of_streams(i, 1)
             if i > 0:
-                centre_and_gain(i - 1, 1)
+                centre_and_gain(i - 1, 0)
             mean(i)
+            if i > 0:
+                centre_and_gain(i - 1, 1)
             if i >= GP_SUMS and i + STREAMS < ROW_TILES:
                 load_streams(i + STREAMS)
-            if i > 0:
-                scale_rows(i - 1, 0)
+            if i == 1:
+                finish(0)
             squares(i)
-            if i > 0:
-                scale_rows(i - 1, 1)
-                bias_store(i - 1)
+            if i > 1:
+                finish(i - 1)
             row_rstd(i)
         for half in range(HALVES):
             centre_and_gain(ROW_TILES - 1, half)

@@ -21,13 +21,15 @@ ROW_TILES = L_TILES * B
 W_GROUPS = D // GROUP
 C_TILES = D // P
 BANK = 512
-HALVES = D // BANK
+BANKS = 8
+HALVES = 2
 EPS = 1e-5
+
 DEPTH = 3
-STREAMS = 5
+AHEAD = BANKS // L_TILES
+STREAMS = 7
 GP_SUMS = 4
-O_BUFS = 6
-LAG = 2
+VECTOR_TAIL = 3
 
 FLOPS = 2 * L * B * D * D
 
@@ -37,23 +39,34 @@ def tile_coattention_pb_kernel(tc, x, res_a, ctx_v, W_v, bn_v_g, bn_v_b, prelu_v
     with ExitStack() as whole:
         whole.enter_context(tc.manual_schedule())
         const = whole.enter_context(tc.tile_pool(name="const", bufs=1))
-        slabs = whole.enter_context(tc.tile_pool(name="slabs", bufs=2 * C_TILES + 1))
+        slabs = whole.enter_context(tc.tile_pool(name="slabs", bufs=2 * C_TILES))
         streams = whole.enter_context(tc.tile_pool(name="streams", bufs=STREAMS))
-        rows_pool = whole.enter_context(tc.tile_pool(name="rows_pool", bufs=O_BUFS))
-        res_pool = whole.enter_context(tc.tile_pool(name="res_pool", bufs=5))
-        junk_pool = whole.enter_context(tc.tile_pool(name="junk_pool", bufs=1))
+        sums = whole.enter_context(tc.tile_pool(name="sums", bufs=6))
+        results = whole.enter_context(tc.tile_pool(name="results", bufs=5))
+        scratch = whole.enter_context(tc.tile_pool(name="scratch", bufs=1))
         mx = whole.enter_context(tc.tile_pool(name="mx", bufs=1))
-        psum = whole.enter_context(tc.psum_pool(name="psum", bufs=8))
+        psum = whole.enter_context(tc.psum_pool(name="psum", bufs=BANKS))
+
+        def bank(name):
+            tile = psum.tile([P, BANK], F32, tag="bank", name=name)
+            return tile
+
+        def col(tile, c):
+            return tile[:, c : c + 1]
+
+        def half_cols(half):
+            return slice(half * BANK, (half + 1) * BANK)
 
         w_rows = [W_v[h * GROUP : (h + 1) * GROUP, :].rearrange("(r p) k -> p r k", p=P) for h in range(W_GROUPS)]
         c_rows = [ctx_v[:, j * P : (j + 1) * P, :].rearrange("b l k -> l b k") for j in range(L_TILES)]
-        sources = w_rows + c_rows
+        sources = [w_rows[0]] + c_rows + [w_rows[1]]
+        LAST = len(sources) - 1
         raw_tiles = {}
 
         def load_group(s):
             raw = slabs.tile([P, TILES, D], BF16, tag="slab", name="raw", align_bytes=64)
-            for hf in range(2):
-                r = slice(2 * hf, 2 * hf + 2)
+            for upper in range(2):
+                r = slice(2 * upper, 2 * upper + 2)
                 nc.sync.dma_start(out=raw[:, r, :], in_=sources[s][:, r, :])
             raw_tiles[s] = raw
 
@@ -80,66 +93,80 @@ def tile_coattention_pb_kernel(tc, x, res_a, ctx_v, W_v, bn_v_g, bn_v_b, prelu_v
         sign = const.tile([P, 1], F32)
         ident_sign = const.tile([P, P], BF16)
         bn_gain_bias = const.tile([P, 2 * C_TILES], F32)
-        ln_gain_bias = const.tile([P, 2 * C_TILES], F32)
         neg_gain = const.tile([P, C_TILES], F32)
+        ln_gain_bias = const.tile([P, 2 * C_TILES], F32)
         ln_bias = const.tile([P, D], F32)
         stats = const.tile([P, C_TILES, L_TILES, 6], F32)
         mean_var = const.tile([P, C_TILES, 2], F32)
         bn_rstd = const.tile([P, C_TILES], F32)
         neg_mean_gain = const.tile([P, C_TILES], F32)
         affine = const.tile([P, C_TILES, 2], F32)
-        row_sum = const.tile([P, ROW_TILES, HALVES], F32)
-        scaled_sums = const.tile([P, ROW_TILES, HALVES], F32)
+        half_sums = const.tile([P, ROW_TILES, HALVES], F32)
+        half_means = const.tile([P, ROW_TILES, HALVES], F32)
         neg_mean = const.tile([P, ROW_TILES], F32)
         sum_sq = const.tile([P, ROW_TILES], F32)
         ln_rstd = const.tile([P, ROW_TILES], F32)
 
+        def prepare_slope():
+            nc.vector.tensor_scalar_add(out=slope_less_1[:], in0=slope[:], scalar1=-1.0)
+            nc.vector.tensor_scalar(out=sign[:], in0=slope_less_1[:], scalar1=0.0, scalar2=2.0, op0=ALU.is_le, op1=ALU.mult)
+            nc.vector.tensor_scalar_add(out=sign[:], in0=sign[:], scalar1=-1.0)
+
+        def prepare_vectors():
+            columns = psum.tile([P, P], BF16, tag="bank", name="columns")
+            nc.tensor.transpose(columns[:], vector_rows[:], ident_bf[:])
+            nc.vector.tensor_copy(out=ln_gain_bias[:], in_=columns[:, 2 * C_TILES : 4 * C_TILES])
+            nc.vector.tensor_scalar_mul(out=bn_gain_bias[:], in0=columns[:, 0 : 2 * C_TILES], scalar1=sign[:])
+            nc.vector.tensor_scalar_mul(out=ident_sign[:], in0=ident_bf[:], scalar1=sign[:])
+            nc.vector.tensor_scalar_mul(out=neg_gain[:], in0=bn_gain_bias[:, 0:C_TILES], scalar1=-1.0)
+
         def spread(name, first):
             tile = bank(name)
             for q in range(TILES):
-                column = ln_gain_bias[:, first + q : first + q + 1].to_broadcast([P, P])
-                nc.tensor.transpose(tile[:, q * P : (q + 1) * P], column, ident[:])
+                repeated = col(ln_gain_bias, first + q).to_broadcast([P, P])
+                nc.tensor.transpose(tile[:, q * P : (q + 1) * P], repeated, ident[:])
             return tile
 
-        def bank(name):
-            tile = psum.tile([P, BANK], F32, tag="bank", name=name)
-            return tile
-
+        staged = {}
         mx_tiles = {}
 
-        def prepare_group(s):
+        def transpose_part(s, g, upper, copy):
+            if s not in staged:
+                grouped = slabs.tile([P, PASSES, GROUP * 4], BF16, tag="slab", name="grouped", align_bytes=64)
+                staged[s] = grouped
+            xt = bank("xt")
+            planes = xt[:].rearrange("p (t u r) -> p t u r", t=2, u=2)
+            for t in range(2):
+                words = raw_tiles[s][:, 2 * upper + t, :].bitcast(F32)
+                for u in range(2):
+                    first = (2 * g + u) * P
+                    nc.tensor.transpose(planes[:, t, u, :], words[:, first : first + P], ident[:])
+            words_out = staged[s][:, g, :].bitcast(F32).rearrange("p (h t r u) -> p h t r u", h=2, t=2, u=2)
+            copy(out=words_out[:, upper, :, :, :], in_=planes.rearrange("p t u r -> p t r u"))
+
+        def quantise(s):
             codes = mx.tile([P, PASSES, GROUP], U32, name="codes%d" % s, align_bytes=64)
             scales = mx.tile([P, PASSES, GROUP], U8, name="scales%d" % s, align_bytes=64)
-            grouped = slabs.tile([P, PASSES, GROUP * 4], BF16, tag="slab", name="grouped", align_bytes=64)
             for g in range(PASSES):
-                words_out = grouped[:, g, :].bitcast(F32).rearrange("p (q r u) -> p q r u", q=2, u=2)
-                for hf in range(2):
-                    xt = bank("xt")
-                    planes = xt[:].rearrange("p (t u r) -> p t u r", t=2, u=2)
-                    for t in range(2):
-                        words = raw_tiles[s][:, 2 * hf + t, :].bitcast(F32)
-                        for u in range(2):
-                            first = (2 * g + u) * P
-                            nc.tensor.transpose(planes[:, t, u, :], words[:, first : first + P], ident[:])
-                    src = planes.rearrange("p t u r -> p t r u")
-                    dst = words_out[:, hf, :, :].rearrange("p (t r) u -> p t r u", t=2)
-                    if g == PASSES - 1 and hf == 0:
-                        nc.vector.tensor_copy(out=dst, in_=src)
-                    else:
-                        nc.scalar.copy(out=dst, in_=src)
-            if s + DEPTH < len(sources):
-                load_group(s + DEPTH)
-            for g in range(PASSES):
-                nc.vector.quantize_mx(out=codes[:, g, :].bitcast(FP8X4), scales=scales[:, g, :], in_=grouped[:, g, :])
+                nc.vector.quantize_mx(out=codes[:, g, :].bitcast(FP8X4), scales=scales[:, g, :], in_=staged[s][:, g, :])
             mx_tiles[s] = (codes, scales)
 
+        def prepare_group(s):
+            for g in range(PASSES):
+                for upper in range(2):
+                    on_vector = g == 1 and upper == 0
+                    transpose_part(s, g, upper, nc.vector.tensor_copy if on_vector else nc.scalar.copy)
+            if s + DEPTH < len(sources):
+                load_group(s + DEPTH)
+            quantise(s)
+
         y_tiles = {}
-        zn = {}
+        terms = {}
 
         def product(ct, j):
             h, q = divmod(ct, TILES)
-            w_codes, w_scales = mx_tiles[h]
-            c_codes, c_scales = mx_tiles[W_GROUPS + j]
+            w_codes, w_scales = mx_tiles[0 if h == 0 else LAST]
+            c_codes, c_scales = mx_tiles[1 + j]
             cols = slice(q * P, (q + 1) * P)
             y = bank("y")
             for g in range(PASSES):
@@ -159,47 +186,44 @@ def tile_coattention_pb_kernel(tc, x, res_a, ctx_v, W_v, bn_v_g, bn_v_b, prelu_v
             if j == L_TILES - 1:
                 nc.vector.bn_aggr(out=mean_var[:, ct, :], in_=stats[:, ct, :, :].rearrange("p j s -> p (j s)"))
 
-        def col(tile, ct):
-            return tile[:, ct : ct + 1]
-
-        def bn_prepare(ct, step):
-            if step == 0:
-                nc.scalar.activation(
-                    out=col(bn_rstd, ct), in_=mean_var[:, ct, 1:2], func=ACT.Abs_reciprocal_sqrt, bias=eps[:], scale=1.0
-                )
-                nc.scalar.activation(out=col(neg_mean_gain, ct), in_=mean_var[:, ct, 0:1], func=ACT.Copy, scale=col(neg_gain, ct))
-            else:
-                rstd = col(bn_rstd, ct)
-                nc.scalar.activation(out=affine[:, ct, 0:1], in_=col(bn_gain_bias, ct), func=ACT.Copy, scale=rstd)
-                nc.scalar.activation(
-                    out=affine[:, ct, 1:2], in_=col(neg_mean_gain, ct), func=ACT.Identity,
-                    bias=col(bn_gain_bias, C_TILES + ct), scale=rstd,
-                )
-
-        def normalise(ct, j):
-            if j % 2 == 0:
-                two = slabs.tile([P, 2, 2, GROUP], F32, tag="slab", name="two", align_bytes=64)
-                zn[ct, j // 2] = two
+        def batch_norm_rstd(ct):
             nc.scalar.activation(
-                out=zn[ct, j // 2][:, 0, j % 2, :], in_=y_tiles[ct, j][:], func=ACT.Identity,
+                out=col(bn_rstd, ct), in_=mean_var[:, ct, 1:2], func=ACT.Abs_reciprocal_sqrt, bias=eps[:], scale=1.0
+            )
+            nc.scalar.activation(out=col(neg_mean_gain, ct), in_=mean_var[:, ct, 0:1], func=ACT.Copy, scale=col(neg_gain, ct))
+
+        def batch_norm_affine(ct):
+            rstd = col(bn_rstd, ct)
+            nc.scalar.activation(out=affine[:, ct, 0:1], in_=col(bn_gain_bias, ct), func=ACT.Copy, scale=rstd)
+            nc.scalar.activation(
+                out=affine[:, ct, 1:2], in_=col(neg_mean_gain, ct), func=ACT.Identity, bias=col(bn_gain_bias, C_TILES + ct), scale=rstd
+            )
+
+        def first_term(ct, j):
+            if j % 2 == 0:
+                pair = slabs.tile([P, 2, 2, GROUP], F32, tag="slab", name="pair", align_bytes=64)
+                terms[ct, j // 2] = pair
+            nc.scalar.activation(
+                out=terms[ct, j // 2][:, 0, j % 2, :], in_=y_tiles[ct, j][:], func=ACT.Identity,
                 bias=affine[:, ct, 1:2], scale=affine[:, ct, 0:1],
             )
 
-        def second_term(ct, jj):
-            two = zn[ct, jj]
-            if (ct, jj) in ((1, 1), (3, 1), (5, 1), (7, 1),):
-                nc.scalar.activation(out=two[:, 1, :, :], in_=two[:, 0, :, :], func=ACT.Relu, scale=slope_less_1[:])
+        def second_term(ct, upper):
+            pair = terms[ct, upper]
+            if upper == 1 and ct % 2 == 1:
+                nc.scalar.activation(out=pair[:, 1, :, :], in_=pair[:, 0, :, :], func=ACT.Relu, scale=slope_less_1[:])
             else:
                 nc.vector.tensor_scalar(
-                    out=two[:, 1, :, :], in0=two[:, 0, :, :], scalar1=slope_less_1[:], scalar2=0.0, op0=ALU.mult, op1=ALU.max
+                    out=pair[:, 1, :, :], in0=pair[:, 0, :, :], scalar1=slope_less_1[:], scalar2=0.0, op0=ALU.mult, op1=ALU.max
                 )
 
         x_tiles = {}
         a_tiles = {}
         o_tiles = {}
-        res_v = {}
+        to_sum = {}
         res_tiles = {}
         ln_gain = {}
+        ln_bias_banks = {}
 
         def load_streams(i):
             j, b = divmod(i, B)
@@ -209,60 +233,62 @@ def tile_coattention_pb_kernel(tc, x, res_a, ctx_v, W_v, bn_v_g, bn_v_b, prelu_v
             nc.sync.dma_start(out=a_t[:], in_=res_a[b, j * P : (j + 1) * P, :])
             x_tiles[i], a_tiles[i] = x_t, a_t
 
-        def add_streams(i):
-            o = rows_pool.tile([P, D], F32, tag="o", name="o")
-            for half in range(HALVES):
-                cols = slice(half * BANK, (half + 1) * BANK)
-                nc.gpsimd.tensor_tensor(out=o[:, cols], in0=x_tiles[i][:, cols], in1=a_tiles[i][:, cols], op=ALU.add)
+        def new_sum(i):
+            o = sums.tile([P, D], F32)
             o_tiles[i] = o
+
+        def add_streams(i):
+            new_sum(i)
+            for half in range(HALVES):
+                cols = half_cols(half)
+                nc.gpsimd.tensor_tensor(out=o_tiles[i][:, cols], in0=x_tiles[i][:, cols], in1=a_tiles[i][:, cols], op=ALU.add)
 
         def to_rows(i, half):
             j, b = divmod(i, B)
             rows = slice(b * P, (b + 1) * P)
-            res = bank("res")
-            if i >= GP_SUMS:
-                a_half = a_tiles[i][:, half * BANK : (half + 1) * BANK]
-                nc.tensor.matmul(res[:], lhsT=ident_sign[:], rhs=a_half, start=True, stop=False)
+            adds_a = i >= GP_SUMS
+            total = bank("total")
+            if adds_a:
+                nc.tensor.matmul(total[:], lhsT=ident_sign[:], rhs=a_tiles[i][:, half_cols(half)], start=True, stop=False)
             for q in range(TILES):
-                two = zn[half * TILES + q, j // 2]
-                cells = res[:, q * P : (q + 1) * P]
-                last = q == TILES - 1 if i >= GP_SUMS else True
-                nc.tensor.matmul(cells, lhsT=two[:, 0, j % 2, rows], rhs=ident[:], is_transpose=True, start=(i < GP_SUMS), stop=False)
-                nc.tensor.matmul(cells, lhsT=two[:, 1, j % 2, rows], rhs=ident[:], is_transpose=True, start=False, stop=last)
-            res_v[i, half] = res
+                pair = terms[half * TILES + q, j // 2]
+                cells = total[:, q * P : (q + 1) * P]
+                closes = q == TILES - 1 or not adds_a
+                nc.tensor.matmul(cells, lhsT=pair[:, 0, j % 2, rows], rhs=ident[:], is_transpose=True, start=not adds_a, stop=False)
+                nc.tensor.matmul(cells, lhsT=pair[:, 1, j % 2, rows], rhs=ident[:], is_transpose=True, start=False, stop=closes)
+            to_sum[i, half] = total
 
         def sum_of_streams(i, half):
-            cols = slice(half * BANK, (half + 1) * BANK)
+            cols = half_cols(half)
             if i < GP_SUMS:
                 other = o_tiles[i]
             else:
                 other = x_tiles[i]
                 if half == 0:
-                    o = rows_pool.tile([P, D], F32, tag="o", name="o")
-                    o_tiles[i] = o
+                    new_sum(i)
             nc.vector.scalar_tensor_tensor(
-                out=o_tiles[i][:, cols], in0=res_v[i, half][:], scalar=sign[:], in1=other[:, cols], op0=ALU.mult, op1=ALU.add,
-                accum_out=row_sum[:, i, half : half + 1],
+                out=o_tiles[i][:, cols], in0=to_sum[i, half][:], scalar=sign[:], in1=other[:, cols], op0=ALU.mult, op1=ALU.add,
+                accum_out=half_sums[:, i, half : half + 1],
             )
 
         def mean(i):
             nc.vector.tensor_scalar(
-                out=scaled_sums[:, i, :], in0=row_sum[:, i, :], scalar1=-1.0 / D, scalar2=None, op0=ALU.mult, op1=ALU.add,
+                out=half_means[:, i, :], in0=half_sums[:, i, :], scalar1=-1.0 / D, scalar2=None, op0=ALU.mult, op1=ALU.add,
                 accum_out=col(neg_mean, i),
             )
 
         def centre_and_gain(i, half):
-            cols = slice(half * BANK, (half + 1) * BANK)
             if half == 0:
-                res = res_pool.tile([P, D], F32)
+                res = results.tile([P, D], F32)
                 res_tiles[i] = res
+            cols = half_cols(half)
             nc.vector.scalar_tensor_tensor(
                 out=res_tiles[i][:, cols], in0=o_tiles[i][:, cols], scalar=col(neg_mean, i), in1=ln_gain[half][:],
                 op0=ALU.add, op1=ALU.mult,
             )
 
         def squares(i):
-            junk = junk_pool.tile([P, D], BF16)
+            junk = scratch.tile([P, D], BF16)
             nc.scalar.activation(
                 out=junk[:], in_=o_tiles[i][:], func=ACT.Square, bias=col(neg_mean, i), scale=1.0, accum_out=col(sum_sq, i)
             )
@@ -275,91 +301,87 @@ def tile_coattention_pb_kernel(tc, x, res_a, ctx_v, W_v, bn_v_g, bn_v_b, prelu_v
         def finish(i):
             j, b = divmod(i, B)
             res = res_tiles[i]
-            pieces = HALVES if i in (0, ROW_TILES - 2) else 1
-            for piece in range(pieces):
-                cols = slice(piece * (D // pieces), (piece + 1) * (D // pieces))
-                nc.scalar.activation(out=res[:, cols], in_=res[:, cols], func=ACT.Copy, scale=col(ln_rstd, i))
-                nc.gpsimd.tensor_tensor(out=res[:, cols], in0=res[:, cols], in1=ln_bias[:, cols], op=ALU.add)
-                nc.sync.dma_start(out=out[j * P : (j + 1) * P, b, cols], in_=res[:, cols])
-
-        def scale_bias_store(i):
-            j, b = divmod(i, B)
-            res = res_tiles[i]
-            for half in range(HALVES):
-                cols = slice(half * BANK, (half + 1) * BANK)
-                nc.vector.scalar_tensor_tensor(
-                    out=res[:, cols], in0=res[:, cols], scalar=col(ln_rstd, i), in1=ln_bias[:, cols], op0=ALU.mult, op1=ALU.add
-                )
+            on_vector = i >= ROW_TILES - VECTOR_TAIL
+            in_halves = on_vector or i in (0, ROW_TILES - VECTOR_TAIL - 1)
+            for cols in (half_cols(0), half_cols(1)) if in_halves else (slice(0, D),):
+                if on_vector:
+                    nc.vector.scalar_tensor_tensor(
+                        out=res[:, cols], in0=res[:, cols], scalar=col(ln_rstd, i), in1=ln_bias_banks[cols.start // BANK][:],
+                        op0=ALU.mult, op1=ALU.add,
+                    )
+                else:
+                    nc.scalar.activation(out=res[:, cols], in_=res[:, cols], func=ACT.Copy, scale=col(ln_rstd, i))
+                    nc.gpsimd.tensor_tensor(out=res[:, cols], in0=res[:, cols], in1=ln_bias[:, cols], op=ALU.add)
                 nc.sync.dma_start(out=out[j * P : (j + 1) * P, b, cols], in_=res[:, cols])
 
         prepare_group(0)
-        nc.vector.tensor_scalar_add(out=slope_less_1[:], in0=slope[:], scalar1=-1.0)
-        nc.vector.tensor_scalar(out=sign[:], in0=slope_less_1[:], scalar1=0.0, scalar2=2.0, op0=ALU.is_le, op1=ALU.mult)
-        vector_cols = psum.tile([P, P], BF16, tag="bank", name="vector_cols")
-        nc.tensor.transpose(vector_cols[:], vector_rows[:], ident_bf[:])
-        nc.vector.tensor_copy(out=ln_gain_bias[:], in_=vector_cols[:, 2 * C_TILES : 4 * C_TILES])
-        nc.vector.tensor_scalar_add(out=sign[:], in0=sign[:], scalar1=-1.0)
+        prepare_slope()
+        prepare_vectors()
         prepare_group(1)
-        nc.vector.tensor_scalar_mul(out=bn_gain_bias[:], in0=vector_cols[:, 0 : 2 * C_TILES], scalar1=sign[:])
-        nc.vector.tensor_scalar_mul(out=ident_sign[:], in0=ident_bf[:], scalar1=sign[:])
-        nc.vector.tensor_scalar_mul(out=neg_gain[:], in0=bn_gain_bias[:, 0:C_TILES], scalar1=-1.0)
         for half in range(HALVES):
-            bias_ps = spread("bias_ps", C_TILES + half * TILES)
-            nc.scalar.copy(out=ln_bias[:, half * BANK : (half + 1) * BANK], in_=bias_ps[:])
-        prepare_group(2)
+            bias_bank = spread("bias_bank", C_TILES + half * TILES)
+            nc.scalar.copy(out=ln_bias[:, half_cols(half)], in_=bias_bank[:])
         for j in range(1, L_TILES):
-            prepare_group(W_GROUPS + j)
+            prepare_group(1 + j)
             product(0, j - 1)
             statistics(0, j - 1)
         for i in range(STREAMS):
             load_streams(i)
+        for g in range(PASSES):
+            for upper in range(2):
+                transpose_part(LAST, g, upper, nc.scalar.copy)
         product(0, L_TILES - 1)
         statistics(0, L_TILES - 1)
-        for step in range(2):
-            bn_prepare(0, step)
+        batch_norm_rstd(0)
+        batch_norm_affine(0)
+        quantise(LAST)
         for j in range(L_TILES):
             product(1, j)
             statistics(1, j)
+
         quantised_word = const.tile([P, 1], U32)
-        nc.gpsimd.tensor_copy(out=quantised_word[:], in_=mx_tiles[len(sources) - 1][0][:, PASSES - 1, GROUP - 1 : GROUP])
+        nc.gpsimd.tensor_copy(out=quantised_word[:], in_=mx_tiles[LAST][0][:, PASSES - 1, GROUP - 1 : GROUP])
         for i in range(GP_SUMS):
             add_streams(i)
             load_streams(i + STREAMS)
-        PRE = {6:[[5,0]],7:[[6,0]]}
-        MID = {7:[[7,0]]}
-        POST = {2:[[0,0]],3:[[1,0],[0,1]],4:[[2,0],[3,0],[1,1]],5:[[4,0],[3,1]],6:[[2,1]],7:[[4,1],[5,1]]}
-        TAIL = [[6,1],[7,1]]
+
+        WAIT = 3
+        made = 0
         for ct in range(C_TILES):
-            for c, jj in PRE.get(ct, ()):
-                second_term(c, jj)
+            if ct == C_TILES - 1:
+                for half in range(HALVES):
+                    ln_gain[half] = spread("gain_bank", half * TILES)
+            if ct >= WAIT:
+                for c in range(made, min(made + 2, ct)):
+                    second_term(c, 0)
+                    made = c + 1
             for j in range(L_TILES):
-                normalise(ct, j)
-                if ct + 2 < C_TILES:
-                    product(ct + 2, j)
-                elif ct + 2 == C_TILES:
+                first_term(ct, j)
+                if ct + AHEAD < C_TILES:
+                    product(ct + AHEAD, j)
+                    statistics(ct + AHEAD, j)
+                elif ct + AHEAD == C_TILES:
                     to_rows(j, 0)
-                if ct + 1 < C_TILES and j > 1:
-                    bn_prepare(ct + 1, j - 2)
-                if ct + 2 < C_TILES:
-                    statistics(ct + 2, j)
-                elif ct + 2 == C_TILES:
                     sum_of_streams(j, 0)
-                if j == 1:
-                    for c, jj in MID.get(ct, ()):
-                        second_term(c, jj)
-            for c, jj in POST.get(ct, ()):
-                second_term(c, jj)
-        for c, jj in TAIL:
-            second_term(c, jj)
+                if ct + 1 < C_TILES and j == 2:
+                    batch_norm_rstd(ct + 1)
+                if ct + 1 < C_TILES and j == 3:
+                    batch_norm_affine(ct + 1)
+                if ct == C_TILES - 1 and j == 1:
+                    second_term(ct, 0)
+            if ct >= WAIT:
+                second_term(ct - WAIT, 1)
+        for c in range(C_TILES - WAIT, C_TILES):
+            second_term(c, 1)
 
         for i in range(ROW_TILES):
-            if i >= B:
+            if i >= L_TILES:
                 to_rows(i, 0)
             to_rows(i, 1)
-            if i == 0:
+            if i == ROW_TILES - VECTOR_TAIL:
                 for half in range(HALVES):
-                    ln_gain[half] = spread("gain", half * TILES)
-            if i >= B:
+                    ln_bias_banks[half] = spread("bias_bank", C_TILES + half * TILES)
+            if i >= L_TILES:
                 sum_of_streams(i, 0)
             sum_of_streams(i, 1)
             if i > 0:
@@ -377,4 +399,4 @@ def tile_coattention_pb_kernel(tc, x, res_a, ctx_v, W_v, bn_v_g, bn_v_b, prelu_v
             row_rstd(i)
         for half in range(HALVES):
             centre_and_gain(ROW_TILES - 1, half)
-        scale_bias_store(ROW_TILES - 1)
+        finish(ROW_TILES - 1)

@@ -16,8 +16,7 @@ L, B, D = 512, 4, 1024
 PASSES = 2
 GROUP = 512
 TILES = GROUP // P
-L_TILES = L // P
-ROW_TILES = L_TILES * B
+ROW_TILES = B * TILES
 W_GROUPS = D // GROUP
 C_TILES = D // P
 BANK = 512
@@ -26,7 +25,7 @@ HALVES = 2
 EPS = 1e-5
 
 DEPTH = 3
-AHEAD = BANKS // L_TILES
+AHEAD = BANKS // B
 STREAMS = 7
 GP_SUMS = 4
 VECTOR_TAIL = 3
@@ -58,7 +57,7 @@ def tile_coattention_pb_kernel(tc, x, res_a, ctx_v, W_v, bn_v_g, bn_v_b, prelu_v
             return slice(half * BANK, (half + 1) * BANK)
 
         w_rows = [W_v[h * GROUP : (h + 1) * GROUP, :].rearrange("(r p) k -> p r k", p=P) for h in range(W_GROUPS)]
-        c_rows = [ctx_v[:, j * P : (j + 1) * P, :].rearrange("b l k -> l b k") for j in range(L_TILES)]
+        c_rows = [ctx_v[j].rearrange("(p r) k -> p r k", r=TILES) for j in range(B)]
         sources = [w_rows[0]] + c_rows + [w_rows[1]]
         LAST = len(sources) - 1
         raw_tiles = {}
@@ -96,7 +95,7 @@ def tile_coattention_pb_kernel(tc, x, res_a, ctx_v, W_v, bn_v_g, bn_v_b, prelu_v
         neg_gain = const.tile([P, C_TILES], F32)
         ln_gain_bias = const.tile([P, 2 * C_TILES], F32)
         ln_bias = const.tile([P, D], F32)
-        stats = const.tile([P, C_TILES, L_TILES, 6], F32)
+        stats = const.tile([P, C_TILES, B, 6], F32)
         mean_var = const.tile([P, C_TILES, 2], F32)
         bn_rstd = const.tile([P, C_TILES], F32)
         neg_mean_gain = const.tile([P, C_TILES], F32)
@@ -183,7 +182,7 @@ def tile_coattention_pb_kernel(tc, x, res_a, ctx_v, W_v, bn_v_g, bn_v_b, prelu_v
 
         def statistics(ct, j):
             nc.vector.bn_stats(out=stats[:, ct, j, :], in_=y_tiles[ct, j][:])
-            if j == L_TILES - 1:
+            if j == B - 1:
                 nc.vector.bn_aggr(out=mean_var[:, ct, :], in_=stats[:, ct, :, :].rearrange("p j s -> p (j s)"))
 
         def batch_norm_rstd(ct):
@@ -210,7 +209,7 @@ def tile_coattention_pb_kernel(tc, x, res_a, ctx_v, W_v, bn_v_g, bn_v_b, prelu_v
 
         def second_term(ct, upper):
             pair = terms[ct, upper]
-            if upper == 1 and ct % 2 == 1:
+            if upper == 1 and (ct == 0 or ct % 2 == 1):
                 nc.scalar.activation(out=pair[:, 1, :, :], in_=pair[:, 0, :, :], func=ACT.Relu, scale=slope_less_1[:])
             else:
                 nc.vector.tensor_scalar(
@@ -226,11 +225,11 @@ def tile_coattention_pb_kernel(tc, x, res_a, ctx_v, W_v, bn_v_g, bn_v_b, prelu_v
         ln_bias_banks = {}
 
         def load_streams(i):
-            j, b = divmod(i, B)
+            j, r = divmod(i, TILES)
             x_t = streams.tile([P, D], BF16)
-            nc.sync.dma_start(out=x_t[:], in_=x[j * P : (j + 1) * P, b, :])
+            nc.sync.dma_start(out=x_t[:], in_=x[:, j, :].rearrange("(p r) c -> r p c", r=TILES)[r])
             a_t = streams.tile([P, D], BF16)
-            nc.sync.dma_start(out=a_t[:], in_=res_a[b, j * P : (j + 1) * P, :])
+            nc.sync.dma_start(out=a_t[:], in_=res_a[j].rearrange("(p r) c -> r p c", r=TILES)[r])
             x_tiles[i], a_tiles[i] = x_t, a_t
 
         def new_sum(i):
@@ -244,8 +243,8 @@ def tile_coattention_pb_kernel(tc, x, res_a, ctx_v, W_v, bn_v_g, bn_v_b, prelu_v
                 nc.gpsimd.tensor_tensor(out=o_tiles[i][:, cols], in0=x_tiles[i][:, cols], in1=a_tiles[i][:, cols], op=ALU.add)
 
         def to_rows(i, half):
-            j, b = divmod(i, B)
-            rows = slice(b * P, (b + 1) * P)
+            j, r = divmod(i, TILES)
+            rows = slice(r * P, (r + 1) * P)
             adds_a = i >= GP_SUMS
             total = bank("total")
             if adds_a:
@@ -299,7 +298,7 @@ def tile_coattention_pb_kernel(tc, x, res_a, ctx_v, W_v, bn_v_g, bn_v_b, prelu_v
             )
 
         def finish(i):
-            j, b = divmod(i, B)
+            j, r = divmod(i, TILES)
             res = res_tiles[i]
             on_vector = i >= ROW_TILES - VECTOR_TAIL
             in_halves = on_vector or i in (0, ROW_TILES - VECTOR_TAIL - 1)
@@ -312,7 +311,7 @@ def tile_coattention_pb_kernel(tc, x, res_a, ctx_v, W_v, bn_v_g, bn_v_b, prelu_v
                 else:
                     nc.scalar.activation(out=res[:, cols], in_=res[:, cols], func=ACT.Copy, scale=col(ln_rstd, i))
                     nc.gpsimd.tensor_tensor(out=res[:, cols], in0=res[:, cols], in1=ln_bias[:, cols], op=ALU.add)
-                nc.sync.dma_start(out=out[j * P : (j + 1) * P, b, cols], in_=res[:, cols])
+                nc.sync.dma_start(out=out[:, j, cols].rearrange("(p r) c -> r p c", r=TILES)[r], in_=res[:, cols])
 
         prepare_group(0)
         prepare_slope()
@@ -321,7 +320,7 @@ def tile_coattention_pb_kernel(tc, x, res_a, ctx_v, W_v, bn_v_g, bn_v_b, prelu_v
         for half in range(HALVES):
             bias_bank = spread("bias_bank", C_TILES + half * TILES)
             nc.scalar.copy(out=ln_bias[:, half_cols(half)], in_=bias_bank[:])
-        for j in range(1, L_TILES):
+        for j in range(1, B):
             prepare_group(1 + j)
             product(0, j - 1)
             statistics(0, j - 1)
@@ -330,12 +329,12 @@ def tile_coattention_pb_kernel(tc, x, res_a, ctx_v, W_v, bn_v_g, bn_v_b, prelu_v
         for g in range(PASSES):
             for upper in range(2):
                 transpose_part(LAST, g, upper, nc.scalar.copy)
-        product(0, L_TILES - 1)
-        statistics(0, L_TILES - 1)
+        product(0, B - 1)
+        statistics(0, B - 1)
         batch_norm_rstd(0)
         batch_norm_affine(0)
         quantise(LAST)
-        for j in range(L_TILES):
+        for j in range(B):
             product(1, j)
             statistics(1, j)
 
@@ -355,7 +354,7 @@ def tile_coattention_pb_kernel(tc, x, res_a, ctx_v, W_v, bn_v_g, bn_v_b, prelu_v
                 for c in range(made, min(made + 2, ct)):
                     second_term(c, 0)
                     made = c + 1
-            for j in range(L_TILES):
+            for j in range(B):
                 first_term(ct, j)
                 if ct + AHEAD < C_TILES:
                     product(ct + AHEAD, j)
@@ -363,9 +362,8 @@ def tile_coattention_pb_kernel(tc, x, res_a, ctx_v, W_v, bn_v_g, bn_v_b, prelu_v
                 elif ct + AHEAD == C_TILES:
                     to_rows(j, 0)
                     sum_of_streams(j, 0)
-                if ct + 1 < C_TILES and j == 2:
-                    batch_norm_rstd(ct + 1)
                 if ct + 1 < C_TILES and j == 3:
+                    batch_norm_rstd(ct + 1)
                     batch_norm_affine(ct + 1)
                 if ct == C_TILES - 1 and j == 1:
                     second_term(ct, 0)
@@ -375,13 +373,13 @@ def tile_coattention_pb_kernel(tc, x, res_a, ctx_v, W_v, bn_v_g, bn_v_b, prelu_v
             second_term(c, 1)
 
         for i in range(ROW_TILES):
-            if i >= L_TILES:
+            if i >= B:
                 to_rows(i, 0)
             to_rows(i, 1)
             if i == ROW_TILES - VECTOR_TAIL:
                 for half in range(HALVES):
                     ln_bias_banks[half] = spread("bias_bank", C_TILES + half * TILES)
-            if i >= L_TILES:
+            if i >= B:
                 sum_of_streams(i, 0)
             sum_of_streams(i, 1)
             if i > 0:
@@ -394,9 +392,11 @@ def tile_coattention_pb_kernel(tc, x, res_a, ctx_v, W_v, bn_v_g, bn_v_b, prelu_v
             if i == 1:
                 finish(0)
             squares(i)
-            if i > 1:
+            if 1 < i <= ROW_TILES - VECTOR_TAIL:
                 finish(i - 1)
             row_rstd(i)
-        for half in range(HALVES):
-            centre_and_gain(ROW_TILES - 1, half)
+        finish(ROW_TILES - 3)
+        finish(ROW_TILES - 2)
+        centre_and_gain(ROW_TILES - 1, 0)
+        centre_and_gain(ROW_TILES - 1, 1)
         finish(ROW_TILES - 1)

@@ -151,8 +151,8 @@ def tile_coattention_pb_kernel(tc, x, res_a, ctx_v, W_v, bn_v_g, bn_v_b, prelu_v
             mx_tiles[s] = (codes, scales)
 
         def prepare_group(s):
-            for g in range(PASSES):
-                for upper in range(2):
+            for upper in range(2):
+                for g in range(PASSES):
                     on_vector = g == 1 and upper == 0
                     transpose_part(s, g, upper, nc.vector.tensor_copy if on_vector else nc.scalar.copy)
             if s + DEPTH < len(sources):
@@ -326,8 +326,8 @@ def tile_coattention_pb_kernel(tc, x, res_a, ctx_v, W_v, bn_v_g, bn_v_b, prelu_v
             statistics(0, j - 1)
         for i in range(STREAMS):
             load_streams(i)
-        for g in range(PASSES):
-            for upper in range(2):
+        for upper in range(2):
+            for g in range(PASSES):
                 transpose_part(LAST, g, upper, nc.scalar.copy)
         product(0, B - 1)
         statistics(0, B - 1)

from contextlib import ExitStack

import concourse.mybir as mybir
from concourse.masks import make_identity

F32 = mybir.dt.float32
BF16 = mybir.dt.bfloat16
U32 = mybir.dt.uint32
U8 = mybir.dt.uint8
FP8X4 = mybir.dt.float8_e4m3fn_x4
ALU = mybir.AluOpType
ACT = mybir.ActivationFunctionType

P = 128
L, B, D = 512, 4, 1024
PASSES = 2
GROUP = 512
TILES = GROUP // P
ROW_TILES = B * TILES
W_GROUPS = D // GROUP
C_TILES = D // P
BANK = 512
BANKS = 8
HALVES = 2
EPS = 1e-5

DEPTH = 3
AHEAD = BANKS // B
STREAMS = 7
GP_SUMS = 4
VECTOR_TAIL = 3

FLOPS = 2 * L * B * D * D


def tile_coattention_pb_kernel(tc, x, res_a, ctx_v, W_v, bn_v_g, bn_v_b, prelu_v, ln_g, ln_b, out):
    nc = tc.nc
    with ExitStack() as whole:
        whole.enter_context(tc.manual_schedule())
        const = whole.enter_context(tc.tile_pool(name="const", bufs=1))
        slabs = whole.enter_context(tc.tile_pool(name="slabs", bufs=2 * C_TILES))
        streams = whole.enter_context(tc.tile_pool(name="streams", bufs=STREAMS))
        sums = whole.enter_context(tc.tile_pool(name="sums", bufs=6))
        results = whole.enter_context(tc.tile_pool(name="results", bufs=5))
        scratch = whole.enter_context(tc.tile_pool(name="scratch", bufs=1))
        mx = whole.enter_context(tc.tile_pool(name="mx", bufs=1))
        psum = whole.enter_context(tc.psum_pool(name="psum", bufs=BANKS))

        def bank(name):
            tile = psum.tile([P, BANK], F32, tag="bank", name=name)
            return tile

        def col(tile, c):
            return tile[:, c : c + 1]

        def half_cols(half):
            return slice(half * BANK, (half + 1) * BANK)

        w_rows = [W_v[h * GROUP : (h + 1) * GROUP, :].rearrange("(r p) k -> p r k", p=P) for h in range(W_GROUPS)]
        c_rows = [ctx_v[j].rearrange("(p r) k -> p r k", r=TILES) for j in range(B)]
        sources = [w_rows[0]] + c_rows + [w_rows[1]]
        LAST = len(sources) - 1
        raw_tiles = {}

        def load_group(s):
            raw = slabs.tile([P, TILES, D], BF16, tag="slab", name="raw", align_bytes=64)
            for upper in range(2):
                r = slice(2 * upper, 2 * upper + 2)
                nc.sync.dma_start(out=raw[:, r, :], in_=sources[s][:, r, :])
            raw_tiles[s] = raw

        for s in range(DEPTH):
            load_group(s)

        ident = const.tile([P, P], F32)
        make_identity(nc, ident[:])
        ident_bf = const.tile([P, P], BF16)
        make_identity(nc, ident_bf[:])
        eps = const.tile([P, 1], F32)
        nc.vector.memset(eps[:], EPS)
        table_first = const.tile([P, 1], F32)
        nc.scalar.activation(out=table_first[:], in_=eps[:], func=ACT.Abs_reciprocal_sqrt)

        vector_rows = const.tile([P, P], BF16)
        nc.vector.memset(vector_rows[:], 0.0)
        slope = const.tile([P, 1], BF16)
        nc.scalar.dma_start(out=slope[:], in_=prelu_v.partition_broadcast(P))
        for v, vector in enumerate((bn_v_g, bn_v_b, ln_g, ln_b)):
            nc.scalar.dma_start(out=vector_rows[v * C_TILES : (v + 1) * C_TILES, :], in_=vector.rearrange("(t c) -> t c", t=C_TILES))

        slope_less_1 = const.tile([P, 1], F32)
        sign = const.tile([P, 1], F32)
        ident_sign = const.tile([P, P], BF16)
        bn_gain_bias = const.tile([P, 2 * C_TILES], F32)
        neg_gain = const.tile([P, C_TILES], F32)
        ln_gain_bias = const.tile([P, 2 * C_TILES], F32)
        ln_bias = const.tile([P, D], F32)
        stats = const.tile([P, C_TILES, B, 6], F32)
        mean_var = const.tile([P, C_TILES, 2], F32)
        bn_rstd = const.tile([P, C_TILES], F32)
        neg_mean_gain = const.tile([P, C_TILES], F32)
        affine = const.tile([P, C_TILES, 2], F32)
        half_sums = const.tile([P, ROW_TILES, HALVES], F32)
        half_means = const.tile([P, ROW_TILES, HALVES], F32)
        neg_mean = const.tile([P, ROW_TILES], F32)
        sum_sq = const.tile([P, ROW_TILES], F32)
        ln_rstd = const.tile([P, ROW_TILES], F32)

        def prepare_slope():
            nc.vector.tensor_scalar_add(out=slope_less_1[:], in0=slope[:], scalar1=-1.0)
            nc.vector.tensor_scalar(out=sign[:], in0=slope_less_1[:], scalar1=0.0, scalar2=2.0, op0=ALU.is_le, op1=ALU.mult)
            nc.vector.tensor_scalar_add(out=sign[:], in0=sign[:], scalar1=-1.0)

        def prepare_vectors():
            columns = psum.tile([P, P], BF16, tag="bank", name="columns")
            nc.tensor.transpose(columns[:], vector_rows[:], ident_bf[:])
            nc.vector.tensor_copy(out=ln_gain_bias[:], in_=columns[:, 2 * C_TILES : 4 * C_TILES])
            nc.vector.tensor_scalar_mul(out=bn_gain_bias[:], in0=columns[:, 0 : 2 * C_TILES], scalar1=sign[:])
            nc.vector.tensor_scalar_mul(out=ident_sign[:], in0=ident_bf[:], scalar1=sign[:])
            nc.vector.tensor_scalar_mul(out=neg_gain[:], in0=bn_gain_bias[:, 0:C_TILES], scalar1=-1.0)

        def spread(name, first):
            tile = bank(name)
            for q in range(TILES):
                repeated = col(ln_gain_bias, first + q).to_broadcast([P, P])
                nc.tensor.transpose(tile[:, q * P : (q + 1) * P], repeated, ident[:])
            return tile

        staged = {}
        mx_tiles = {}

        def transpose_part(s, g, upper, copy):
            if s not in staged:
                grouped = slabs.tile([P, PASSES, GROUP * 4], BF16, tag="slab", name="grouped", align_bytes=64)
                staged[s] = grouped
            xt = bank("xt")
            planes = xt[:].rearrange("p (t u r) -> p t u r", t=2, u=2)
            for t in range(2):
                words = raw_tiles[s][:, 2 * upper + t, :].bitcast(F32)
                for u in range(2):
                    first = (2 * g + u) * P
                    nc.tensor.transpose(planes[:, t, u, :], words[:, first : first + P], ident[:])
            words_out = staged[s][:, g, :].bitcast(F32).rearrange("p (h t r u) -> p h t r u", h=2, t=2, u=2)
            copy(out=words_out[:, upper, :, :, :], in_=planes.rearrange("p t u r -> p t r u"))

        def quantise(s):
            codes = mx.tile([P, PASSES, GROUP], U32, name="codes%d" % s, align_bytes=64)
            scales = mx.tile([P, PASSES, GROUP], U8, name="scales%d" % s, align_bytes=64)
            for g in range(PASSES):
                nc.vector.quantize_mx(out=codes[:, g, :].bitcast(FP8X4), scales=scales[:, g, :], in_=staged[s][:, g, :])
            mx_tiles[s] = (codes, scales)

        def prepare_group(s):
            for upper in range(2):
                for g in range(PASSES):
                    on_vector = g == 1 and upper == 0
                    transpose_part(s, g, upper, nc.vector.tensor_copy if on_vector else nc.scalar.copy)
            if s + DEPTH < len(sources):
                load_group(s + DEPTH)
            quantise(s)

        y_tiles = {}
        terms = {}

        def product(ct, j):
            h, q = divmod(ct, TILES)
            w_codes, w_scales = mx_tiles[0 if h == 0 else LAST]
            c_codes, c_scales = mx_tiles[1 + j]
            cols = slice(q * P, (q + 1) * P)
            y = bank("y")
            for g in range(PASSES):
                nc.tensor.matmul_mx(
                    out=y[:],
                    lhsT=w_codes[:, g, cols].bitcast(FP8X4),
                    lhsT_scale=w_scales[:, g, cols],
                    rhs=c_codes[:, g, :].bitcast(FP8X4),
                    rhs_scale=c_scales[:, g, :],
                    start=(g == 0),
                    stop=(g == PASSES - 1),
                )
            y_tiles[ct, j] = y

        def statistics(ct, j):
            nc.vector.bn_stats(out=stats[:, ct, j, :], in_=y_tiles[ct, j][:])
            if j == B - 1:
                nc.vector.bn_aggr(out=mean_var[:, ct, :], in_=stats[:, ct, :, :].rearrange("p j s -> p (j s)"))

        def batch_norm_rstd(ct):
            nc.scalar.activation(
                out=col(bn_rstd, ct), in_=mean_var[:, ct, 1:2], func=ACT.Abs_reciprocal_sqrt, bias=eps[:], scale=1.0
            )
            nc.scalar.activation(out=col(neg_mean_gain, ct), in_=mean_var[:, ct, 0:1], func=ACT.Copy, scale=col(neg_gain, ct))

        def batch_norm_affine(ct):
            rstd = col(bn_rstd, ct)
            nc.scalar.activation(out=affine[:, ct, 0:1], in_=col(bn_gain_bias, ct), func=ACT.Copy, scale=rstd)
            nc.scalar.activation(
                out=affine[:, ct, 1:2], in_=col(neg_mean_gain, ct), func=ACT.Identity, bias=col(bn_gain_bias, C_TILES + ct), scale=rstd
            )

        def first_term(ct, j):
            if j % 2 == 0:
                pair = slabs.tile([P, 2, 2, GROUP], F32, tag="slab", name="pair", align_bytes=64)
                terms[ct, j // 2] = pair
            nc.scalar.activation(
                out=terms[ct, j // 2][:, 0, j % 2, :], in_=y_tiles[ct, j][:], func=ACT.Identity,
                bias=affine[:, ct, 1:2], scale=affine[:, ct, 0:1],
            )

        def second_term(ct, upper):
            pair = terms[ct, upper]
            if upper == 1 and (ct == 0 or ct % 2 == 1):
                nc.scalar.activation(out=pair[:, 1, :, :], in_=pair[:, 0, :, :], func=ACT.Relu, scale=slope_less_1[:])
            else:
                nc.vector.tensor_scalar(
                    out=pair[:, 1, :, :], in0=pair[:, 0, :, :], scalar1=slope_less_1[:], scalar2=0.0, op0=ALU.mult, op1=ALU.max
                )

        x_tiles = {}
        a_tiles = {}
        o_tiles = {}
        to_sum = {}
        res_tiles = {}
        ln_gain = {}
        ln_bias_banks = {}

        def load_streams(i):
            j, r = divmod(i, TILES)
            x_t = streams.tile([P, D], BF16)
            nc.sync.dma_start(out=x_t[:], in_=x[:, j, :].rearrange("(p r) c -> r p c", r=TILES)[r])
            a_t = streams.tile([P, D], BF16)
            nc.sync.dma_start(out=a_t[:], in_=res_a[j].rearrange("(p r) c -> r p c", r=TILES)[r])
            x_tiles[i], a_tiles[i] = x_t, a_t

        def new_sum(i):
            o = sums.tile([P, D], F32)
            o_tiles[i] = o

        def add_streams(i):
            new_sum(i)
            for half in range(HALVES):
                cols = half_cols(half)
                nc.gpsimd.tensor_tensor(out=o_tiles[i][:, cols], in0=x_tiles[i][:, cols], in1=a_tiles[i][:, cols], op=ALU.add)

        def to_rows(i, half):
            j, r = divmod(i, TILES)
            rows = slice(r * P, (r + 1) * P)
            adds_a = i >= GP_SUMS
            total = bank("total")
            if adds_a:
                nc.tensor.matmul(total[:], lhsT=ident_sign[:], rhs=a_tiles[i][:, half_cols(half)], start=True, stop=False)
            for q in range(TILES):
                pair = terms[half * TILES + q, j // 2]
                cells = total[:, q * P : (q + 1) * P]
                closes = q == TILES - 1 or not adds_a
                nc.tensor.matmul(cells, lhsT=pair[:, 0, j % 2, rows], rhs=ident[:], is_transpose=True, start=not adds_a, stop=False)
                nc.tensor.matmul(cells, lhsT=pair[:, 1, j % 2, rows], rhs=ident[:], is_transpose=True, start=False, stop=closes)
            to_sum[i, half] = total

        def sum_of_streams(i, half):
            cols = half_cols(half)
            if i < GP_SUMS:
                other = o_tiles[i]
            else:
                other = x_tiles[i]
                if half == 0:
                    new_sum(i)
            nc.vector.scalar_tensor_tensor(
                out=o_tiles[i][:, cols], in0=to_sum[i, half][:], scalar=sign[:], in1=other[:, cols], op0=ALU.mult, op1=ALU.add,
                accum_out=half_sums[:, i, half : half + 1],
            )

        def mean(i):
            nc.vector.tensor_scalar(
                out=half_means[:, i, :], in0=half_sums[:, i, :], scalar1=-1.0 / D, scalar2=None, op0=ALU.mult, op1=ALU.add,
                accum_out=col(neg_mean, i),
            )

        def centre_and_gain(i, half):
            if half == 0:
                res = results.tile([P, D], F32)
                res_tiles[i] = res
            cols = half_cols(half)
            nc.vector.scalar_tensor_tensor(
                out=res_tiles[i][:, cols], in0=o_tiles[i][:, cols], scalar=col(neg_mean, i), in1=ln_gain[half][:],
                op0=ALU.add, op1=ALU.mult,
            )

        def squares(i):
            junk = scratch.tile([P, D], BF16)
            nc.scalar.activation(
                out=junk[:], in_=o_tiles[i][:], func=ACT.Square, bias=col(neg_mean, i), scale=1.0, accum_out=col(sum_sq, i)
            )

        def row_rstd(i):
            nc.scalar.activation(
                out=col(ln_rstd, i), in_=col(sum_sq, i), func=ACT.Abs_reciprocal_sqrt, bias=eps[:], scale=1.0 / D
            )

        def finish(i):
            j, r = divmod(i, TILES)
            res = res_tiles[i]
            on_vector = i >= ROW_TILES - VECTOR_TAIL
            in_halves = on_vector or i in (0, ROW_TILES - VECTOR_TAIL - 1)
            for cols in (half_cols(0), half_cols(1)) if in_halves else (slice(0, D),):
                if on_vector:
                    nc.vector.scalar_tensor_tensor(
                        out=res[:, cols], in0=res[:, cols], scalar=col(ln_rstd, i), in1=ln_bias_banks[cols.start // BANK][:],
                        op0=ALU.mult, op1=ALU.add,
                    )
                else:
                    nc.scalar.activation(out=res[:, cols], in_=res[:, cols], func=ACT.Copy, scale=col(ln_rstd, i))
                    nc.gpsimd.tensor_tensor(out=res[:, cols], in0=res[:, cols], in1=ln_bias[:, cols], op=ALU.add)
                nc.sync.dma_start(out=out[:, j, cols].rearrange("(p r) c -> r p c", r=TILES)[r], in_=res[:, cols])

        prepare_group(0)
        prepare_slope()
        prepare_vectors()
        prepare_group(1)
        for half in range(HALVES):
            bias_bank = spread("bias_bank", C_TILES + half * TILES)
            nc.scalar.copy(out=ln_bias[:, half_cols(half)], in_=bias_bank[:])
        for j in range(1, B):
            prepare_group(1 + j)
            product(0, j - 1)
            statistics(0, j - 1)
        for i in range(STREAMS):
            load_streams(i)
        for upper in range(2):
            for g in range(PASSES):
                transpose_part(LAST, g, upper, nc.scalar.copy)
        product(0, B - 1)
        statistics(0, B - 1)
        batch_norm_rstd(0)
        batch_norm_affine(0)
        quantise(LAST)
        for j in range(B):
            product(1, j)
            statistics(1, j)

        quantised_word = const.tile([P, 1], U32)
        nc.gpsimd.tensor_copy(out=quantised_word[:], in_=mx_tiles[LAST][0][:, PASSES - 1, GROUP - 1 : GROUP])
        for i in range(GP_SUMS):
            add_streams(i)
            load_streams(i + STREAMS)

        WAIT = 3
        made = 0
        for ct in range(C_TILES):
            if ct == C_TILES - 1:
                for half in range(HALVES):
                    ln_gain[half] = spread("gain_bank", half * TILES)
            if ct >= WAIT:
                for c in range(made, min(made + 2, ct)):
                    second_term(c, 0)
                    made = c + 1
            for j in range(B):
                first_term(ct, j)
                if ct + AHEAD < C_TILES:
                    product(ct + AHEAD, j)
                    statistics(ct + AHEAD, j)
                elif ct + AHEAD == C_TILES:
                    to_rows(j, 0)
                    sum_of_streams(j, 0)
                if ct + 1 < C_TILES and j == 3:
                    batch_norm_rstd(ct + 1)
                    batch_norm_affine(ct + 1)
                if ct == C_TILES - 1 and j == 1:
                    second_term(ct, 0)
            if ct >= WAIT:
                second_term(ct - WAIT, 1)
        for c in range(C_TILES - WAIT, C_TILES):
            second_term(c, 1)

        for i in range(ROW_TILES):
            if i >= B:
                to_rows(i, 0)
            to_rows(i, 1)
            if i == ROW_TILES - VECTOR_TAIL:
                for half in range(HALVES):
                    ln_bias_banks[half] = spread("bias_bank", C_TILES + half * TILES)
            if i >= B:
                sum_of_streams(i, 0)
            sum_of_streams(i, 1)
            if i > 0:
                centre_and_gain(i - 1, 0)
            mean(i)
            if i > 0:
                centre_and_gain(i - 1, 1)
            if i >= GP_SUMS and i + STREAMS < ROW_TILES:
                load_streams(i + STREAMS)
            if i == 1:
                finish(0)
            squares(i)
            if 1 < i <= ROW_TILES - VECTOR_TAIL:
                finish(i - 1)
            row_rstd(i)
        finish(ROW_TILES - 3)
        finish(ROW_TILES - 2)
        centre_and_gain(ROW_TILES - 1, 0)
        centre_and_gain(ROW_TILES - 1, 1)
        finish(ROW_TILES - 1)
